import numpy as np
import ml_dtypes


def mxq(x, axis, fmt="e4m3"):
    dtype, down = {"e4m3": (ml_dtypes.float8_e4m3fn, 7), "e5m2": (ml_dtypes.float8_e5m2, 14)}[fmt]
    v = np.moveaxis(np.asarray(x, np.float32).astype(ml_dtypes.bfloat16).astype(np.float64), axis, -1)
    blocks = v.reshape(v.shape[:-1] + (-1, 32))
    amax = np.abs(blocks).max(-1, keepdims=True)
    byte = np.maximum(np.where(amax > 0, np.frexp(amax)[1] - 1 + 127, 0) - down, 1)
    scale = np.exp2(byte - 127.0)
    codes = (blocks / scale).astype(np.float32).astype(dtype).astype(np.float64)
    return np.moveaxis((codes * scale).reshape(v.shape), -1, axis)


WIDE = False


def mx_kscale(k):
    if not WIDE:
        return np.ones(k)
    levels = np.array([10, -10, 5, -5, 0])
    a = np.random.permutation(np.resize(levels, k // 512 * 4)).reshape(k // 512, 4)
    idx = np.arange(k)
    return np.exp2(a[idx // 512, idx % 128 // 32])


BF16 = ml_dtypes.bfloat16


def bf(x):
    return np.asarray(x, np.float32).astype(BF16)


def f64(x):
    return np.asarray(x).astype(np.float64)


B, T, D, H, G, HD, W = 1, 512, 2560, 8, 4, 256, 256
EPS = 1e-6


def rmsnorm(u, w):
    var = np.mean(u * u, axis=-1, keepdims=True)
    return u * (1.0 / np.sqrt(var + EPS)) * (1.0 + w)


def setup_inputs():
    s = mx_kscale(D)
    return {"x": bf(np.random.standard_normal((B, T, D)) * s),
            "Wq": bf(np.random.standard_normal((D, H * HD)) * 0.005 / np.sqrt(D) / s[:, None]),
            "Wk": bf(np.random.standard_normal((D, G * HD)) * 0.005 / np.sqrt(D) / s[:, None]),
            "Wv": bf(np.random.standard_normal((D, G * HD)) * 1.0 / np.sqrt(D) / s[:, None]),
            "q_scale": bf(np.random.standard_normal(HD) * 0.2),
            "k_scale": bf(np.random.standard_normal(HD) * 0.2)}


def reference(x, Wq, Wk, Wv, q_scale, k_scale):
    xq = mxq(f64(x), 2, "e4m3")
    q = (xq @ mxq(f64(Wq), 0, "e4m3")).reshape(B, T, H, HD).transpose(0, 2, 1, 3)
    k = (xq @ mxq(f64(Wk), 0, "e4m3")).reshape(B, T, G, HD).transpose(0, 2, 1, 3)
    v = (xq @ mxq(f64(Wv), 0, "e4m3")).reshape(B, T, G, HD).transpose(0, 2, 1, 3)
    return rmsnorm(q, f64(q_scale)), rmsnorm(k, f64(k_scale)), v

@@ -1,0 +1,186 @@
+from contextlib import ExitStack
+
+import concourse.mybir as mybir
+from concourse.masks import make_identity
+
+F32 = mybir.dt.float32
+BF16 = mybir.dt.bfloat16
+U32 = mybir.dt.uint32
+U8 = mybir.dt.uint8
+FP8X4 = mybir.dt.float8_e4m3fn_x4
+ACT = mybir.ActivationFunctionType
+ALU = mybir.AluOpType
+
+P = 128
+PACK = 4
+K_PASS = P * PACK
+TOKENS = 512
+TOKEN_TILES = TOKENS // P
+D_MODEL = 2560
+PASSES = D_MODEL // K_PASS
+HEAD = 256
+BANK = 512
+HEADS_PER_BANK = BANK // HEAD
+GROUP = 1024
+HALVES = GROUP // BANK
+EPS = 1e-6
+VECTOR_COLS = 576
+
+FLOPS = 2 * TOKENS * D_MODEL * 4096
+
+
+def tile_groupedqueryattention_pa_kernel(
+    tc, x, Wq, Wk, Wv, q_scale, k_scale, out_0, out_1, out_2
+):
+    nc = tc.nc
+    with ExitStack() as ctx:
+        const = ctx.enter_context(tc.tile_pool(name="const", bufs=1))
+        xpool = ctx.enter_context(tc.tile_pool(name="xpool", bufs=1))
+        raw_pool = ctx.enter_context(tc.tile_pool(name="raw", bufs=6))
+        grouped_pool = ctx.enter_context(tc.tile_pool(name="grouped", bufs=3))
+        codes_pool = ctx.enter_context(tc.tile_pool(name="codes", bufs=5))
+        stage_pool = ctx.enter_context(tc.tile_pool(name="stage", bufs=3))
+        squares_pool = ctx.enter_context(tc.tile_pool(name="squares", bufs=2))
+        small = ctx.enter_context(tc.tile_pool(name="small", bufs=3))
+        psum = ctx.enter_context(tc.psum_pool(name="psum", bufs=8))
+
+        x_raw = xpool.tile([P, TOKEN_TILES, D_MODEL], BF16)
+        x_rows = x[0].rearrange("(p i) k -> p i k", i=TOKEN_TILES)
+        first_k = 2 * K_PASS
+        nc.sync.dma_start(out=x_raw[:, :, 0:first_k], in_=x_rows[:, :, 0:first_k])
+
+        scale_rows = const.tile([P, 2 * HEAD], BF16)
+        nc.vector.memset(scale_rows[:], 0.0)
+        nc.sync.dma_start(out=scale_rows[0:1, 0:HEAD], in_=q_scale.unsqueeze(0))
+        nc.sync.dma_start(out=scale_rows[0:1, HEAD:], in_=k_scale.unsqueeze(0))
+        nc.sync.dma_start(out=x_raw[:, :, first_k:], in_=x_rows[:, :, first_k:])
+
+        ident = const.tile([P, P], F32)
+        make_identity(nc, ident[:])
+        eps = const.tile([P, 1], F32)
+        nc.vector.memset(eps[:], EPS)
+        ones = const.tile([P, P], BF16)
+        nc.vector.memset(ones[:], 1.0)
+        spread = psum.tile([P, BANK], F32, tag="bank")
+        nc.tensor.matmul(out=spread[:], lhsT=ones[:], rhs=scale_rows[:], start=True, stop=True)
+        gain = const.tile([P, 2 * HEAD], F32)
+        nc.vector.tensor_scalar_add(out=gain[:], in0=spread[:], scalar1=1.0)
+
+        x_grouped = xpool.tile([P, PASSES, TOKENS * PACK], BF16, align_bytes=64)
+        x_codes = xpool.tile([P, PASSES, TOKENS], U32, align_bytes=64)
+        x_scales = xpool.tile([P, PASSES, TOKENS], U8, align_bytes=64)
+        for g in range(PASSES):
+            for pair in range(TOKEN_TILES // 2):
+                xt = psum.tile([P, 2, 2 * P], F32, tag="bank")
+                for u in range(2):
+                    for half in range(2):
+                        i = 2 * pair + half
+                        words = x_raw[:, i, g * K_PASS : (g + 1) * K_PASS].bitcast(F32)
+                        nc.tensor.transpose(
+                            xt[:, u, half * P : (half + 1) * P],
+                            words.rearrange("p (q u) -> p q u", u=2)[:, :, u],
+                            ident[:],
+                        )
+                columns = x_grouped[:, g, pair * 2 * P * PACK : (pair + 1) * 2 * P * PACK]
+                target = columns.bitcast(F32).rearrange("p (r u) -> p r u", u=2)
+                source = xt[:].rearrange("p u r -> p r u")
+                if pair == 0:
+                    nc.scalar.copy(out=target, in_=source)
+                else:
+                    nc.vector.tensor_copy(out=target, in_=source)
+            nc.vector.quantize_mx(
+                out=x_codes[:, g, :].bitcast(FP8X4),
+                scales=x_scales[:, g, :],
+                in_=x_grouped[:, g, :],
+            )
+
+        rounds = [
+            (Wq[:, 0:GROUP], out_0[0, 0:4], gain[:, 0:HEAD]),
+            (Wq[:, GROUP : 2 * GROUP], out_0[0, 4:8], gain[:, 0:HEAD]),
+            (Wk, out_1[0], gain[:, HEAD:]),
+            (Wv, out_2[0], None),
+        ]
+        for w_cols, out_heads, head_gain in rounds:
+            acc = [
+                [psum.tile([P, BANK], F32, tag="bank", name="acc") for i in range(TOKEN_TILES)]
+                for j in range(HALVES)
+            ]
+            for g in range(PASSES):
+                raw = raw_pool.tile([P, PACK, GROUP], BF16)
+                nc.sync.dma_start(
+                    out=raw[:],
+                    in_=w_cols[g * K_PASS : (g + 1) * K_PASS, :].rearrange(
+                        "(p t) c -> p t c", t=PACK
+                    ),
+                )
+                grouped = grouped_pool.tile([P, GROUP, PACK], BF16, align_bytes=64)
+                nc.vector.tensor_copy(
+                    out=grouped[:, 0:VECTOR_COLS, :].rearrange("p (c i) t -> p c t i", i=4),
+                    in_=raw[:, :, 0:VECTOR_COLS].rearrange("p t (c i) -> p c t i", i=4),
+                )
+                nc.scalar.copy(
+                    out=grouped[:, VECTOR_COLS:, :].rearrange("p (c i) t -> p c t i", i=4),
+                    in_=raw[:, :, VECTOR_COLS:].rearrange("p t (c i) -> p c t i", i=4),
+                )
+                codes = codes_pool.tile([P, GROUP], U32, align_bytes=64)
+                scales = codes_pool.tile([P, GROUP], U8, align_bytes=64)
+                for j in range(HALVES):
+                    cols = slice(j * BANK, (j + 1) * BANK)
+                    nc.vector.quantize_mx(
+                        out=codes[:, cols].bitcast(FP8X4),
+                        scales=scales[:, cols],
+                        in_=grouped[:, cols, :].rearrange("p c t -> p (c t)"),
+                    )
+                    for i in range(TOKEN_TILES):
+                        tokens = slice(i * P, (i + 1) * P)
+                        nc.tensor.matmul_mx(
+                            out=acc[j][i][:],
+                            lhsT=x_codes[:, g, tokens].bitcast(FP8X4),
+                            lhsT_scale=x_scales[:, g, tokens],
+                            rhs=codes[:, cols].bitcast(FP8X4),
+                            rhs_scale=scales[:, cols],
+                            start=(g == 0),
+                            stop=(g == PASSES - 1),
+                        )
+
+            for j in range(HALVES):
+                stage = stage_pool.tile([P, HEADS_PER_BANK, TOKEN_TILES, HEAD], F32)
+                if head_gain is None:
+                    for i in range(TOKEN_TILES):
+                        target = stage[:, :, i, :]
+                        source = acc[j][i][:].rearrange("p (h d) -> p h d", h=HEADS_PER_BANK)
+                        if i % 2 == 0:
+                            nc.scalar.copy(out=target, in_=source)
+                        else:
+                            nc.vector.tensor_copy(out=target, in_=source)
+                else:
+                    pieces = [(i, h) for i in range(TOKEN_TILES) for h in range(HEADS_PER_BANK)]
+                    sumsq = small.tile([P, len(pieces)], F32)
+                    squares = squares_pool.tile([P, len(pieces), HEAD], BF16)
+                    for n, (i, h) in enumerate(pieces):
+                        nc.scalar.activation(
+                            out=squares[:, n, :],
+                            in_=acc[j][i][:, h * HEAD : (h + 1) * HEAD],
+                            func=ACT.Square,
+                            accum_out=sumsq[:, n : n + 1],
+                        )
+                    rms = small.tile([P, len(pieces)], F32)
+                    nc.scalar.activation(
+                        out=rms[:], in_=sumsq[:], func=ACT.Sqrt, scale=1.0 / HEAD, bias=eps[:]
+                    )
+                    inv_rms = small.tile([P, len(pieces)], F32)
+                    nc.vector.reciprocal(out=inv_rms[:], in_=rms[:])
+                    for n, (i, h) in enumerate(pieces):
+                        nc.vector.scalar_tensor_tensor(
+                            out=stage[:, h, i, :],
+                            in0=acc[j][i][:, h * HEAD : (h + 1) * HEAD],
+                            scalar=inv_rms[:, n : n + 1],
+                            in1=head_gain,
+                            op0=ALU.mult,
+                            op1=ALU.mult,
+                        )
+                heads = out_heads[j * HEADS_PER_BANK : (j + 1) * HEADS_PER_BANK]
+                nc.sync.dma_start(
+                    out=heads.rearrange("h (p i) d -> p h (i d)", i=TOKEN_TILES),
+                    in_=stage[:].rearrange("p h i d -> p h (i d)"),
+                )

@@ -20,11 +20,16 @@ D_MODEL = 2560
 PASSES = D_MODEL // K_PASS
 HEAD = 256
 BANK = 512
-HEADS_PER_BANK = BANK // HEAD
-GROUP = 1024
-HALVES = GROUP // BANK
+HEADS = BANK // HEAD
+SLAB = 2 * BANK
 EPS = 1e-6
-VECTOR_COLS = 576
+VECTOR_COLS = 240
+RAW_BUFS = 10
+FIRST_X_PASSES = 2
+REGROUP_AHEAD = 3
+QUANTISE_AHEAD = 2
+X_AHEAD = 4
+EMPTY_DELAY = 2
 
 FLOPS = 2 * TOKENS * D_MODEL * 4096
 
@@ -36,40 +41,164 @@ def tile_groupedqueryattention_pa_kernel(
     with ExitStack() as ctx:
         const = ctx.enter_context(tc.tile_pool(name="const", bufs=1))
         xpool = ctx.enter_context(tc.tile_pool(name="xpool", bufs=1))
-        raw_pool = ctx.enter_context(tc.tile_pool(name="raw", bufs=6))
-        grouped_pool = ctx.enter_context(tc.tile_pool(name="grouped", bufs=3))
-        codes_pool = ctx.enter_context(tc.tile_pool(name="codes", bufs=5))
+        raw_pool = ctx.enter_context(tc.tile_pool(name="raw", bufs=RAW_BUFS))
+        grouped_pool = ctx.enter_context(tc.tile_pool(name="grouped", bufs=4))
+        codes_pool = ctx.enter_context(tc.tile_pool(name="codes", bufs=6))
         stage_pool = ctx.enter_context(tc.tile_pool(name="stage", bufs=3))
         squares_pool = ctx.enter_context(tc.tile_pool(name="squares", bufs=2))
         small = ctx.enter_context(tc.tile_pool(name="small", bufs=3))
         psum = ctx.enter_context(tc.psum_pool(name="psum", bufs=8))
+        ctx.enter_context(tc.manual_schedule())
+
+        gain = const.tile([P, 2 * HEAD], F32)
+        groups = [
+            (Wq[:, 0:SLAB], out_0[0, 0:4], gain[:, 0:HEAD]),
+            (Wq[:, SLAB : 2 * SLAB], out_0[0, 4:8], gain[:, 0:HEAD]),
+            (Wk, out_1[0], gain[:, HEAD:]),
+            (Wv, out_2[0], None),
+        ]
+        units = [(j, g) for g in range(PASSES) for j in range(2)]
+        for c in range(1, len(groups)):
+            units.extend([(2 * c + j, g) for j in range(2) for g in range(PASSES)])
+        last_step = {n: rho for n, (rho, g) in enumerate(units) if g == PASSES - 1}
+        slabs = len(groups) * PASSES
+        raw_tiles = {}
+        grouped_tiles = {}
+        code_tiles = {}
+        acc_tiles = {}
+        rms_tiles = {}
+
+        def load(s):
+            w_cols = groups[s // PASSES][0]
+            g = s % PASSES
+            raw = raw_pool.tile([P, PACK, SLAB], BF16)
+            nc.sync.dma_start(
+                out=raw[:],
+                in_=w_cols[g * K_PASS : (g + 1) * K_PASS, :].rearrange("(p t) c -> p t c", t=PACK),
+            )
+            raw_tiles[s] = raw
+
+        def regroup(n):
+            rho, g = units[n]
+            s = (rho // 2) * PASSES + g
+            first = (rho % 2) * BANK
+            raw = raw_tiles[s]
+            grouped = grouped_pool.tile([P, BANK, PACK], BF16, align_bytes=64)
+            nc.vector.tensor_copy(
+                out=grouped[:, 0:VECTOR_COLS, :].rearrange("p (c i) t -> p c t i", i=4),
+                in_=raw[:, :, first : first + VECTOR_COLS].rearrange("p t (c i) -> p c t i", i=4),
+            )
+            nc.scalar.copy(
+                out=grouped[:, VECTOR_COLS:, :].rearrange("p (c i) t -> p c t i", i=4),
+                in_=raw[:, :, first + VECTOR_COLS : first + BANK].rearrange(
+                    "p t (c i) -> p c t i", i=4
+                ),
+            )
+            grouped_tiles[n] = grouped
+            if rho % 2 == 1 and s + RAW_BUFS < slabs:
+                load(s + RAW_BUFS)
+
+        def quantise(n):
+            codes = codes_pool.tile([P, BANK], U32, align_bytes=64)
+            scales = codes_pool.tile([P, BANK], U8, align_bytes=64)
+            nc.vector.quantize_mx(
+                out=codes[:].bitcast(FP8X4),
+                scales=scales[:],
+                in_=grouped_tiles[n][:].rearrange("p c t -> p (c t)"),
+            )
+            code_tiles[n] = (codes, scales)
+
+        def multiply(n):
+            rho, g = units[n]
+            codes, scales = code_tiles[n]
+            for i in range(TOKEN_TILES):
+                if g == 0:
+                    acc = psum.tile([P, BANK], F32, tag="bank")
+                    acc_tiles[(rho, i)] = acc
+                tokens = slice(i * P, (i + 1) * P)
+                nc.tensor.matmul_mx(
+                    out=acc_tiles[(rho, i)][:],
+                    lhsT=x_codes[:, g, tokens].bitcast(FP8X4),
+                    lhsT_scale=x_scales[:, g, tokens],
+                    rhs=codes[:].bitcast(FP8X4),
+                    rhs_scale=scales[:],
+                    start=(g == 0),
+                    stop=(g == PASSES - 1),
+                )
+
+        pieces = [(i, h) for i in range(TOKEN_TILES) for h in range(HEADS)]
+
+        def root_mean_squares(rho):
+            sumsq = small.tile([P, len(pieces)], F32)
+            squares = squares_pool.tile([P, len(pieces), HEAD], BF16)
+            for m, (i, h) in enumerate(pieces):
+                nc.scalar.activation(
+                    out=squares[:, m, :],
+                    in_=acc_tiles[(rho, i)][:, h * HEAD : (h + 1) * HEAD],
+                    func=ACT.Square,
+                    accum_out=sumsq[:, m : m + 1],
+                )
+            rms = small.tile([P, len(pieces)], F32)
+            nc.scalar.activation(
+                out=rms[:], in_=sumsq[:], func=ACT.Sqrt, scale=1.0 / HEAD, bias=eps[:]
+            )
+            rms_tiles[rho] = rms
+
+        def empty(rho):
+            w_cols, out_heads, head_gain = groups[rho // 2]
+            stage = stage_pool.tile([P, HEADS, TOKEN_TILES, HEAD], F32)
+            if head_gain is None:
+                for i in range(TOKEN_TILES):
+                    target = stage[:, :, i, :]
+                    source = acc_tiles[(rho, i)][:].rearrange("p (h d) -> p h d", h=HEADS)
+                    if i % 2 == 0:
+                        nc.scalar.copy(out=target, in_=source)
+                    else:
+                        nc.vector.tensor_copy(out=target, in_=source)
+            else:
+                inv_rms = small.tile([P, len(pieces)], F32)
+                nc.vector.reciprocal(out=inv_rms[:], in_=rms_tiles[rho][:])
+                for m, (i, h) in enumerate(pieces):
+                    nc.vector.scalar_tensor_tensor(
+                        out=stage[:, h, i, :],
+                        in0=acc_tiles[(rho, i)][:, h * HEAD : (h + 1) * HEAD],
+                        scalar=inv_rms[:, m : m + 1],
+                        in1=head_gain,
+                        op0=ALU.mult,
+                        op1=ALU.mult,
+                    )
+            heads = out_heads[(rho % 2) * HEADS : (rho % 2 + 1) * HEADS]
+            nc.sync.dma_start(
+                out=heads.rearrange("h (p i) d -> p h (i d)", i=TOKEN_TILES),
+                in_=stage[:].rearrange("p h i d -> p h (i d)"),
+            )
 
         x_raw = xpool.tile([P, TOKEN_TILES, D_MODEL], BF16)
         x_rows = x[0].rearrange("(p i) k -> p i k", i=TOKEN_TILES)
-        first_k = 2 * K_PASS
+        first_k = FIRST_X_PASSES * K_PASS
         nc.sync.dma_start(out=x_raw[:, :, 0:first_k], in_=x_rows[:, :, 0:first_k])
-
         scale_rows = const.tile([P, 2 * HEAD], BF16)
         nc.vector.memset(scale_rows[:], 0.0)
         nc.sync.dma_start(out=scale_rows[0:1, 0:HEAD], in_=q_scale.unsqueeze(0))
         nc.sync.dma_start(out=scale_rows[0:1, HEAD:], in_=k_scale.unsqueeze(0))
         nc.sync.dma_start(out=x_raw[:, :, first_k:], in_=x_rows[:, :, first_k:])
+        for s in range(RAW_BUFS):
+            load(s)
 
         ident = const.tile([P, P], F32)
         make_identity(nc, ident[:])
         eps = const.tile([P, 1], F32)
         nc.vector.memset(eps[:], EPS)
+        first_sqrt = const.tile([P, 1], F32)
+        nc.scalar.activation(out=first_sqrt[:], in_=eps[:], func=ACT.Sqrt)
         ones = const.tile([P, P], BF16)
         nc.vector.memset(ones[:], 1.0)
-        spread = psum.tile([P, BANK], F32, tag="bank")
-        nc.tensor.matmul(out=spread[:], lhsT=ones[:], rhs=scale_rows[:], start=True, stop=True)
-        gain = const.tile([P, 2 * HEAD], F32)
-        nc.vector.tensor_scalar_add(out=gain[:], in0=spread[:], scalar1=1.0)
 
         x_grouped = xpool.tile([P, PASSES, TOKENS * PACK], BF16, align_bytes=64)
         x_codes = xpool.tile([P, PASSES, TOKENS], U32, align_bytes=64)
         x_scales = xpool.tile([P, PASSES, TOKENS], U8, align_bytes=64)
-        for g in range(PASSES):
+
+        def prepare_x(g):
             for pair in range(TOKEN_TILES // 2):
                 xt = psum.tile([P, 2, 2 * P], F32, tag="bank")
                 for u in range(2):
@@ -94,93 +223,23 @@ def tile_groupedqueryattention_pa_kernel(
                 in_=x_grouped[:, g, :],
             )
 
-        rounds = [
-            (Wq[:, 0:GROUP], out_0[0, 0:4], gain[:, 0:HEAD]),
-            (Wq[:, GROUP : 2 * GROUP], out_0[0, 4:8], gain[:, 0:HEAD]),
-            (Wk, out_1[0], gain[:, HEAD:]),
-            (Wv, out_2[0], None),
-        ]
-        for w_cols, out_heads, head_gain in rounds:
-            acc = [
-                [psum.tile([P, BANK], F32, tag="bank", name="acc") for i in range(TOKEN_TILES)]
-                for j in range(HALVES)
-            ]
-            for g in range(PASSES):
-                raw = raw_pool.tile([P, PACK, GROUP], BF16)
-                nc.sync.dma_start(
-                    out=raw[:],
-                    in_=w_cols[g * K_PASS : (g + 1) * K_PASS, :].rearrange(
-                        "(p t) c -> p t c", t=PACK
-                    ),
-                )
-                grouped = grouped_pool.tile([P, GROUP, PACK], BF16, align_bytes=64)
-                nc.vector.tensor_copy(
-                    out=grouped[:, 0:VECTOR_COLS, :].rearrange("p (c i) t -> p c t i", i=4),
-                    in_=raw[:, :, 0:VECTOR_COLS].rearrange("p t (c i) -> p c t i", i=4),
-                )
-                nc.scalar.copy(
-                    out=grouped[:, VECTOR_COLS:, :].rearrange("p (c i) t -> p c t i", i=4),
-                    in_=raw[:, :, VECTOR_COLS:].rearrange("p t (c i) -> p c t i", i=4),
-                )
-                codes = codes_pool.tile([P, GROUP], U32, align_bytes=64)
-                scales = codes_pool.tile([P, GROUP], U8, align_bytes=64)
-                for j in range(HALVES):
-                    cols = slice(j * BANK, (j + 1) * BANK)
-                    nc.vector.quantize_mx(
-                        out=codes[:, cols].bitcast(FP8X4),
-                        scales=scales[:, cols],
-                        in_=grouped[:, cols, :].rearrange("p c t -> p (c t)"),
-                    )
-                    for i in range(TOKEN_TILES):
-                        tokens = slice(i * P, (i + 1) * P)
-                        nc.tensor.matmul_mx(
-                            out=acc[j][i][:],
-                            lhsT=x_codes[:, g, tokens].bitcast(FP8X4),
-                            lhsT_scale=x_scales[:, g, tokens],
-                            rhs=codes[:, cols].bitcast(FP8X4),
-                            rhs_scale=scales[:, cols],
-                            start=(g == 0),
-                            stop=(g == PASSES - 1),
-                        )
+        for g in range(FIRST_X_PASSES):
+            prepare_x(g)
 
-            for j in range(HALVES):
-                stage = stage_pool.tile([P, HEADS_PER_BANK, TOKEN_TILES, HEAD], F32)
-                if head_gain is None:
-                    for i in range(TOKEN_TILES):
-                        target = stage[:, :, i, :]
-                        source = acc[j][i][:].rearrange("p (h d) -> p h d", h=HEADS_PER_BANK)
-                        if i % 2 == 0:
-                            nc.scalar.copy(out=target, in_=source)
-                        else:
-                            nc.vector.tensor_copy(out=target, in_=source)
-                else:
-                    pieces = [(i, h) for i in range(TOKEN_TILES) for h in range(HEADS_PER_BANK)]
-                    sumsq = small.tile([P, len(pieces)], F32)
-                    squares = squares_pool.tile([P, len(pieces), HEAD], BF16)
-                    for n, (i, h) in enumerate(pieces):
-                        nc.scalar.activation(
-                            out=squares[:, n, :],
-                            in_=acc[j][i][:, h * HEAD : (h + 1) * HEAD],
-                            func=ACT.Square,
-                            accum_out=sumsq[:, n : n + 1],
-                        )
-                    rms = small.tile([P, len(pieces)], F32)
-                    nc.scalar.activation(
-                        out=rms[:], in_=sumsq[:], func=ACT.Sqrt, scale=1.0 / HEAD, bias=eps[:]
-                    )
-                    inv_rms = small.tile([P, len(pieces)], F32)
-                    nc.vector.reciprocal(out=inv_rms[:], in_=rms[:])
-                    for n, (i, h) in enumerate(pieces):
-                        nc.vector.scalar_tensor_tensor(
-                            out=stage[:, h, i, :],
-                            in0=acc[j][i][:, h * HEAD : (h + 1) * HEAD],
-                            scalar=inv_rms[:, n : n + 1],
-                            in1=head_gain,
-                            op0=ALU.mult,
-                            op1=ALU.mult,
-                        )
-                heads = out_heads[j * HEADS_PER_BANK : (j + 1) * HEADS_PER_BANK]
-                nc.sync.dma_start(
-                    out=heads.rearrange("h (p i) d -> p h (i d)", i=TOKEN_TILES),
-                    in_=stage[:].rearrange("p h i d -> p h (i d)"),
-                )
+        spread = psum.tile([P, BANK], F32, tag="bank")
+        nc.tensor.matmul(out=spread[:], lhsT=ones[:], rhs=scale_rows[:], start=True, stop=True)
+        nc.vector.tensor_scalar_add(out=gain[:], in0=spread[:], scalar1=1.0)
+
+        for n in range(-REGROUP_AHEAD, len(units) + EMPTY_DELAY + 1):
+            if FIRST_X_PASSES <= n + X_AHEAD < PASSES:
+                prepare_x(n + X_AHEAD)
+            if n + REGROUP_AHEAD < len(units):
+                regroup(n + REGROUP_AHEAD)
+            if n - EMPTY_DELAY in last_step:
+                empty(last_step[n - EMPTY_DELAY])
+            if 0 <= n + QUANTISE_AHEAD < len(units):
+                quantise(n + QUANTISE_AHEAD)
+            if 0 <= n < len(units):
+                multiply(n)
+                if n in last_step and groups[last_step[n] // 2][2] is not None:
+                    root_mean_squares(last_step[n])

@@ -42,13 +42,12 @@ def tile_groupedqueryattention_pa_kernel(
         const = ctx.enter_context(tc.tile_pool(name="const", bufs=1))
         xpool = ctx.enter_context(tc.tile_pool(name="xpool", bufs=1))
         raw_pool = ctx.enter_context(tc.tile_pool(name="raw", bufs=RAW_BUFS))
-        grouped_pool = ctx.enter_context(tc.tile_pool(name="grouped", bufs=4))
-        codes_pool = ctx.enter_context(tc.tile_pool(name="codes", bufs=6))
+        grouped_pool = ctx.enter_context(tc.tile_pool(name="grouped", bufs=6))
+        codes_pool = ctx.enter_context(tc.tile_pool(name="codes", bufs=8))
         stage_pool = ctx.enter_context(tc.tile_pool(name="stage", bufs=3))
         squares_pool = ctx.enter_context(tc.tile_pool(name="squares", bufs=2))
         small = ctx.enter_context(tc.tile_pool(name="small", bufs=3))
         psum = ctx.enter_context(tc.psum_pool(name="psum", bufs=8))
-        ctx.enter_context(tc.manual_schedule())
 
         gain = const.tile([P, 2 * HEAD], F32)
         groups = [

@@ -23,13 +23,10 @@ BANK = 512
 HEADS = BANK // HEAD
 SLAB = 2 * BANK
 EPS = 1e-6
-VECTOR_COLS = 240
+VECTOR_SHARE = 32
 RAW_BUFS = 10
-FIRST_X_PASSES = 2
-REGROUP_AHEAD = 3
-QUANTISE_AHEAD = 2
-X_AHEAD = 4
-EMPTY_DELAY = 2
+REGROUP_AHEAD = 2
+QUANTISE_AHEAD = 1
 
 FLOPS = 2 * TOKENS * D_MODEL * 4096
 
@@ -41,8 +38,9 @@ def tile_groupedqueryattention_pa_kernel(
     with ExitStack() as ctx:
         const = ctx.enter_context(tc.tile_pool(name="const", bufs=1))
         xpool = ctx.enter_context(tc.tile_pool(name="xpool", bufs=1))
+        xg_pool = ctx.enter_context(tc.tile_pool(name="xgrouped", bufs=2))
         raw_pool = ctx.enter_context(tc.tile_pool(name="raw", bufs=RAW_BUFS))
-        grouped_pool = ctx.enter_context(tc.tile_pool(name="grouped", bufs=6))
+        grouped_pool = ctx.enter_context(tc.tile_pool(name="grouped", bufs=3))
         codes_pool = ctx.enter_context(tc.tile_pool(name="codes", bufs=8))
         stage_pool = ctx.enter_context(tc.tile_pool(name="stage", bufs=3))
         squares_pool = ctx.enter_context(tc.tile_pool(name="squares", bufs=2))
@@ -51,65 +49,74 @@ def tile_groupedqueryattention_pa_kernel(
 
         gain = const.tile([P, 2 * HEAD], F32)
         groups = [
+            (Wk, out_1[0], gain[:, HEAD:]),
             (Wq[:, 0:SLAB], out_0[0, 0:4], gain[:, 0:HEAD]),
             (Wq[:, SLAB : 2 * SLAB], out_0[0, 4:8], gain[:, 0:HEAD]),
-            (Wk, out_1[0], gain[:, HEAD:]),
             (Wv, out_2[0], None),
         ]
-        units = [(j, g) for g in range(PASSES) for j in range(2)]
-        for c in range(1, len(groups)):
-            units.extend([(2 * c + j, g) for j in range(2) for g in range(PASSES)])
-        last_step = {n: rho for n, (rho, g) in enumerate(units) if g == PASSES - 1}
+        last_group = len(groups) - 1
         slabs = len(groups) * PASSES
+        jobs = [(0, 0, BANK), (0, BANK, BANK)]
+        for s in range(1, last_group * PASSES):
+            jobs.append((s, 0, SLAB))
+        for j in range(2):
+            for g in range(PASSES):
+                jobs.append((last_group * PASSES + g, j * BANK, BANK))
         raw_tiles = {}
         grouped_tiles = {}
         code_tiles = {}
         acc_tiles = {}
         rms_tiles = {}
 
-        def load(s):
+        def load(s, pieces=1):
             w_cols = groups[s // PASSES][0]
             g = s % PASSES
             raw = raw_pool.tile([P, PACK, SLAB], BF16)
-            nc.sync.dma_start(
-                out=raw[:],
-                in_=w_cols[g * K_PASS : (g + 1) * K_PASS, :].rearrange("(p t) c -> p t c", t=PACK),
-            )
+            width = SLAB // pieces
+            for n in range(pieces):
+                cols = slice(n * width, (n + 1) * width)
+                nc.sync.dma_start(
+                    out=raw[:, :, cols],
+                    in_=w_cols[g * K_PASS : (g + 1) * K_PASS, cols].rearrange(
+                        "(p t) c -> p t c", t=PACK
+                    ),
+                )
             raw_tiles[s] = raw
 
-        def regroup(n):
-            rho, g = units[n]
-            s = (rho // 2) * PASSES + g
-            first = (rho % 2) * BANK
+        def regroup(m):
+            s, first, width = jobs[m]
             raw = raw_tiles[s]
-            grouped = grouped_pool.tile([P, BANK, PACK], BF16, align_bytes=64)
+            split = width * VECTOR_SHARE // 64
+            grouped = grouped_pool.tile([P, width, PACK], BF16, align_bytes=64)
             nc.vector.tensor_copy(
-                out=grouped[:, 0:VECTOR_COLS, :].rearrange("p (c i) t -> p c t i", i=4),
-                in_=raw[:, :, first : first + VECTOR_COLS].rearrange("p t (c i) -> p c t i", i=4),
+                out=grouped[:, 0:split, :].rearrange("p (c i) t -> p c t i", i=4),
+                in_=raw[:, :, first : first + split].rearrange("p t (c i) -> p c t i", i=4),
             )
             nc.scalar.copy(
-                out=grouped[:, VECTOR_COLS:, :].rearrange("p (c i) t -> p c t i", i=4),
-                in_=raw[:, :, first + VECTOR_COLS : first + BANK].rearrange(
+                out=grouped[:, split:, :].rearrange("p (c i) t -> p c t i", i=4),
+                in_=raw[:, :, first + split : first + width].rearrange(
                     "p t (c i) -> p c t i", i=4
                 ),
             )
-            grouped_tiles[n] = grouped
-            if rho % 2 == 1 and s + RAW_BUFS < slabs:
+            grouped_tiles[m] = grouped
+            if first + width == SLAB and s + RAW_BUFS < slabs:
                 load(s + RAW_BUFS)
 
-        def quantise(n):
-            codes = codes_pool.tile([P, BANK], U32, align_bytes=64)
-            scales = codes_pool.tile([P, BANK], U8, align_bytes=64)
+        def quantise(m):
+            s, first, width = jobs[m]
+            codes = codes_pool.tile([P, width], U32, align_bytes=64)
+            scales = codes_pool.tile([P, width], U8, align_bytes=64)
             nc.vector.quantize_mx(
                 out=codes[:].bitcast(FP8X4),
                 scales=scales[:],
-                in_=grouped_tiles[n][:].rearrange("p c t -> p (c t)"),
+                in_=grouped_tiles[m][:].rearrange("p c t -> p (c t)"),
             )
-            code_tiles[n] = (codes, scales)
+            for c in range(0, width, BANK):
+                rho = 2 * (s // PASSES) + (first + c) // BANK
+                code_tiles[(rho, s % PASSES)] = (codes[:, c : c + BANK], scales[:, c : c + BANK])
 
-        def multiply(n):
-            rho, g = units[n]
-            codes, scales = code_tiles[n]
+        def multiply(rho, g):
+            codes, scales = code_tiles[(rho, g)]
             for i in range(TOKEN_TILES):
                 if g == 0:
                     acc = psum.tile([P, BANK], F32, tag="bank")
@@ -119,8 +126,8 @@ def tile_groupedqueryattention_pa_kernel(
                     out=acc_tiles[(rho, i)][:],
                     lhsT=x_codes[:, g, tokens].bitcast(FP8X4),
                     lhsT_scale=x_scales[:, g, tokens],
-                    rhs=codes[:].bitcast(FP8X4),
-                    rhs_scale=scales[:],
+                    rhs=codes.bitcast(FP8X4),
+                    rhs_scale=scales,
                     start=(g == 0),
                     stop=(g == PASSES - 1),
                 )
@@ -129,10 +136,10 @@ def tile_groupedqueryattention_pa_kernel(
 
         def root_mean_squares(rho):
             sumsq = small.tile([P, len(pieces)], F32)
-            squares = squares_pool.tile([P, len(pieces), HEAD], BF16)
             for m, (i, h) in enumerate(pieces):
+                squares = squares_pool.tile([P, HEAD], BF16)
                 nc.scalar.activation(
-                    out=squares[:, m, :],
+                    out=squares[:],
                     in_=acc_tiles[(rho, i)][:, h * HEAD : (h + 1) * HEAD],
                     func=ACT.Square,
                     accum_out=sumsq[:, m : m + 1],
@@ -146,6 +153,9 @@ def tile_groupedqueryattention_pa_kernel(
         def empty(rho):
             w_cols, out_heads, head_gain = groups[rho // 2]
             stage = stage_pool.tile([P, HEADS, TOKEN_TILES, HEAD], F32)
+            heads = out_heads[(rho % 2) * HEADS : (rho % 2 + 1) * HEADS].rearrange(
+                "h (p i) d -> p h i d", i=TOKEN_TILES
+            )
             if head_gain is None:
                 for i in range(TOKEN_TILES):
                     target = stage[:, :, i, :]
@@ -154,6 +164,9 @@ def tile_groupedqueryattention_pa_kernel(
                         nc.scalar.copy(out=target, in_=source)
                     else:
                         nc.vector.tensor_copy(out=target, in_=source)
+                    if i % 2 == 1:
+                        two = slice(i - 1, i + 1)
+                        nc.sync.dma_start(out=heads[:, :, two, :], in_=stage[:, :, two, :])
             else:
                 inv_rms = small.tile([P, len(pieces)], F32)
                 nc.vector.reciprocal(out=inv_rms[:], in_=rms_tiles[rho][:])
@@ -166,22 +179,21 @@ def tile_groupedqueryattention_pa_kernel(
                         op0=ALU.mult,
                         op1=ALU.mult,
                     )
-            heads = out_heads[(rho % 2) * HEADS : (rho % 2 + 1) * HEADS]
-            nc.sync.dma_start(
-                out=heads.rearrange("h (p i) d -> p h (i d)", i=TOKEN_TILES),
-                in_=stage[:].rearrange("p h i d -> p h (i d)"),
-            )
+                nc.sync.dma_start(out=heads, in_=stage[:])
 
         x_raw = xpool.tile([P, TOKEN_TILES, D_MODEL], BF16)
         x_rows = x[0].rearrange("(p i) k -> p i k", i=TOKEN_TILES)
-        first_k = FIRST_X_PASSES * K_PASS
+        first_k = 2 * K_PASS
+        load(0, pieces=2)
+        load(1)
         nc.sync.dma_start(out=x_raw[:, :, 0:first_k], in_=x_rows[:, :, 0:first_k])
         scale_rows = const.tile([P, 2 * HEAD], BF16)
         nc.vector.memset(scale_rows[:], 0.0)
         nc.sync.dma_start(out=scale_rows[0:1, 0:HEAD], in_=q_scale.unsqueeze(0))
         nc.sync.dma_start(out=scale_rows[0:1, HEAD:], in_=k_scale.unsqueeze(0))
+        load(2)
         nc.sync.dma_start(out=x_raw[:, :, first_k:], in_=x_rows[:, :, first_k:])
-        for s in range(RAW_BUFS):
+        for s in range(3, RAW_BUFS):
             load(s)
 
         ident = const.tile([P, P], F32)
@@ -193,11 +205,11 @@ def tile_groupedqueryattention_pa_kernel(
         ones = const.tile([P, P], BF16)
         nc.vector.memset(ones[:], 1.0)
 
-        x_grouped = xpool.tile([P, PASSES, TOKENS * PACK], BF16, align_bytes=64)
         x_codes = xpool.tile([P, PASSES, TOKENS], U32, align_bytes=64)
         x_scales = xpool.tile([P, PASSES, TOKENS], U8, align_bytes=64)
 
         def prepare_x(g):
+            x_grouped = xg_pool.tile([P, TOKENS * PACK], BF16, align_bytes=64)
             for pair in range(TOKEN_TILES // 2):
                 xt = psum.tile([P, 2, 2 * P], F32, tag="bank")
                 for u in range(2):
@@ -209,36 +221,47 @@ def tile_groupedqueryattention_pa_kernel(
                             words.rearrange("p (q u) -> p q u", u=2)[:, :, u],
                             ident[:],
                         )
-                columns = x_grouped[:, g, pair * 2 * P * PACK : (pair + 1) * 2 * P * PACK]
+                columns = x_grouped[:, pair * 2 * P * PACK : (pair + 1) * 2 * P * PACK]
                 target = columns.bitcast(F32).rearrange("p (r u) -> p r u", u=2)
-                source = xt[:].rearrange("p u r -> p r u")
-                if pair == 0:
-                    nc.scalar.copy(out=target, in_=source)
-                else:
-                    nc.vector.tensor_copy(out=target, in_=source)
+                nc.scalar.copy(out=target, in_=xt[:].rearrange("p u r -> p r u"))
             nc.vector.quantize_mx(
                 out=x_codes[:, g, :].bitcast(FP8X4),
                 scales=x_scales[:, g, :],
-                in_=x_grouped[:, g, :],
+                in_=x_grouped[:],
             )
 
-        for g in range(FIRST_X_PASSES):
-            prepare_x(g)
+        def spread_gains():
+            spread = psum.tile([P, BANK], F32, tag="bank")
+            nc.tensor.matmul(out=spread[:], lhsT=ones[:], rhs=scale_rows[:], start=True, stop=True)
+            nc.vector.tensor_scalar_add(out=gain[:], in0=spread[:], scalar1=1.0)
 
-        spread = psum.tile([P, BANK], F32, tag="bank")
-        nc.tensor.matmul(out=spread[:], lhsT=ones[:], rhs=scale_rows[:], start=True, stop=True)
-        nc.vector.tensor_scalar_add(out=gain[:], in0=spread[:], scalar1=1.0)
-
-        for n in range(-REGROUP_AHEAD, len(units) + EMPTY_DELAY + 1):
-            if FIRST_X_PASSES <= n + X_AHEAD < PASSES:
-                prepare_x(n + X_AHEAD)
-            if n + REGROUP_AHEAD < len(units):
-                regroup(n + REGROUP_AHEAD)
-            if n - EMPTY_DELAY in last_step:
-                empty(last_step[n - EMPTY_DELAY])
-            if 0 <= n + QUANTISE_AHEAD < len(units):
-                quantise(n + QUANTISE_AHEAD)
-            if 0 <= n < len(units):
-                multiply(n)
-                if n in last_step and groups[last_step[n] // 2][2] is not None:
-                    root_mean_squares(last_step[n])
+        order = [(rho, g) for rho in range(2 * len(groups)) for g in range(PASSES)]
+        done = 0
+        waiting = []
+        for m in range(-REGROUP_AHEAD, len(jobs) + 2):
+            if m + REGROUP_AHEAD < len(jobs):
+                regroup(m + REGROUP_AHEAD)
+            ready = [rho for rho, step in waiting if step <= m]
+            waiting = [(rho, step) for rho, step in waiting if step > m]
+            for rho in ready:
+                empty(rho)
+            if 0 <= m + QUANTISE_AHEAD < len(jobs):
+                quantise(m + QUANTISE_AHEAD)
+            if m == 0:
+                prepare_x(0)
+                prepare_x(1)
+                spread_gains()
+            if m == 1:
+                for g in range(2, PASSES):
+                    prepare_x(g)
+            while m >= 1 and done < len(order) and order[done] in code_tiles:
+                rho, g = order[done]
+                s, first, width = jobs[min(m, len(jobs) - 1)]
+                multiply(rho, g)
+                done += 1
+                if g == PASSES - 1:
+                    if groups[rho // 2][2] is not None:
+                        root_mean_squares(rho)
+                        waiting.append((rho, m + 1))
+                    else:
+                        waiting.append((rho, m + 1))

@@ -23,8 +23,8 @@ BANK = 512
 HEADS = BANK // HEAD
 SLAB = 2 * BANK
 EPS = 1e-6
-VECTOR_SHARE = 32
-RAW_BUFS = 10
+VECTOR_SHARE = 33
+RAW_BUFS = {SLAB: 8, BANK: 2}
 REGROUP_AHEAD = 2
 QUANTISE_AHEAD = 1
 
@@ -39,8 +39,8 @@ def tile_groupedqueryattention_pa_kernel(
         const = ctx.enter_context(tc.tile_pool(name="const", bufs=1))
         xpool = ctx.enter_context(tc.tile_pool(name="xpool", bufs=1))
         xg_pool = ctx.enter_context(tc.tile_pool(name="xgrouped", bufs=2))
-        raw_pool = ctx.enter_context(tc.tile_pool(name="raw", bufs=RAW_BUFS))
-        grouped_pool = ctx.enter_context(tc.tile_pool(name="grouped", bufs=3))
+        raw_pool = ctx.enter_context(tc.tile_pool(name="raw", bufs=2))
+        grouped_pool = ctx.enter_context(tc.tile_pool(name="grouped", bufs=4))
         codes_pool = ctx.enter_context(tc.tile_pool(name="codes", bufs=8))
         stage_pool = ctx.enter_context(tc.tile_pool(name="stage", bufs=3))
         squares_pool = ctx.enter_context(tc.tile_pool(name="squares", bufs=2))
@@ -56,51 +56,51 @@ def tile_groupedqueryattention_pa_kernel(
         ]
         last_group = len(groups) - 1
         slabs = len(groups) * PASSES
+        rounds = [(c, first, BANK) for c in range(last_group) for first in (0, BANK)]
+        rounds += [(last_group, 0, BANK), (last_group, BANK, HEAD), (last_group, BANK + HEAD, HEAD)]
         jobs = [(0, 0, BANK), (0, BANK, BANK)]
         for s in range(1, last_group * PASSES):
             jobs.append((s, 0, SLAB))
-        for j in range(2):
+        for c, first, width in rounds[2 * last_group :]:
             for g in range(PASSES):
-                jobs.append((last_group * PASSES + g, j * BANK, BANK))
+                jobs.append((c * PASSES + g, first, width))
         raw_tiles = {}
         grouped_tiles = {}
         code_tiles = {}
         acc_tiles = {}
         rms_tiles = {}
 
-        def load(s, pieces=1):
+        def load(s, first=0, width=SLAB):
             w_cols = groups[s // PASSES][0]
             g = s % PASSES
-            raw = raw_pool.tile([P, PACK, SLAB], BF16)
-            width = SLAB // pieces
-            for n in range(pieces):
-                cols = slice(n * width, (n + 1) * width)
-                nc.sync.dma_start(
-                    out=raw[:, :, cols],
-                    in_=w_cols[g * K_PASS : (g + 1) * K_PASS, cols].rearrange(
-                        "(p t) c -> p t c", t=PACK
-                    ),
-                )
-            raw_tiles[s] = raw
+            raw = raw_pool.tile([P, PACK, width], BF16, tag=f"raw{width}", bufs=RAW_BUFS[width])
+            nc.sync.dma_start(
+                out=raw[:],
+                in_=w_cols[g * K_PASS : (g + 1) * K_PASS, first : first + width].rearrange(
+                    "(p t) c -> p t c", t=PACK
+                ),
+            )
+            for c in range(first, first + width, HEAD):
+                raw_tiles[(s, c)] = raw[:, :, c - first :]
 
         def regroup(m):
             s, first, width = jobs[m]
-            raw = raw_tiles[s]
+            raw = raw_tiles[(s, first)]
             split = width * VECTOR_SHARE // 64
             grouped = grouped_pool.tile([P, width, PACK], BF16, align_bytes=64)
             nc.vector.tensor_copy(
                 out=grouped[:, 0:split, :].rearrange("p (c i) t -> p c t i", i=4),
-                in_=raw[:, :, first : first + split].rearrange("p t (c i) -> p c t i", i=4),
+                in_=raw[:, :, 0:split].rearrange("p t (c i) -> p c t i", i=4),
             )
             nc.scalar.copy(
                 out=grouped[:, split:, :].rearrange("p (c i) t -> p c t i", i=4),
-                in_=raw[:, :, first + split : first + width].rearrange(
+                in_=raw[:, :, split:width].rearrange(
                     "p t (c i) -> p c t i", i=4
                 ),
             )
             grouped_tiles[m] = grouped
-            if first + width == SLAB and s + RAW_BUFS < slabs:
-                load(s + RAW_BUFS)
+            if s > 0 and first + width == SLAB and s + RAW_BUFS[SLAB] < slabs:
+                load(s + RAW_BUFS[SLAB])
 
         def quantise(m):
             s, first, width = jobs[m]
@@ -111,23 +111,23 @@ def tile_groupedqueryattention_pa_kernel(
                 scales=scales[:],
                 in_=grouped_tiles[m][:].rearrange("p c t -> p (c t)"),
             )
-            for c in range(0, width, BANK):
-                rho = 2 * (s // PASSES) + (first + c) // BANK
-                code_tiles[(rho, s % PASSES)] = (codes[:, c : c + BANK], scales[:, c : c + BANK])
+            for c in range(0, width, HEAD):
+                code_tiles[(s, first + c)] = (codes[:, c:], scales[:, c:])
 
         def multiply(rho, g):
-            codes, scales = code_tiles[(rho, g)]
+            c, first, width = rounds[rho]
+            codes, scales = code_tiles[(c * PASSES + g, first)]
             for i in range(TOKEN_TILES):
                 if g == 0:
-                    acc = psum.tile([P, BANK], F32, tag="bank")
+                    acc = psum.tile([P, width], F32, tag="bank")
                     acc_tiles[(rho, i)] = acc
                 tokens = slice(i * P, (i + 1) * P)
                 nc.tensor.matmul_mx(
                     out=acc_tiles[(rho, i)][:],
                     lhsT=x_codes[:, g, tokens].bitcast(FP8X4),
                     lhsT_scale=x_scales[:, g, tokens],
-                    rhs=codes.bitcast(FP8X4),
-                    rhs_scale=scales,
+                    rhs=codes[:, 0:width].bitcast(FP8X4),
+                    rhs_scale=scales[:, 0:width],
                     start=(g == 0),
                     stop=(g == PASSES - 1),
                 )
@@ -151,15 +151,17 @@ def tile_groupedqueryattention_pa_kernel(
             rms_tiles[rho] = rms
 
         def empty(rho):
-            w_cols, out_heads, head_gain = groups[rho // 2]
-            stage = stage_pool.tile([P, HEADS, TOKEN_TILES, HEAD], F32)
-            heads = out_heads[(rho % 2) * HEADS : (rho % 2 + 1) * HEADS].rearrange(
+            c, first, width = rounds[rho]
+            w_cols, out_heads, head_gain = groups[c]
+            n_heads = width // HEAD
+            stage = stage_pool.tile([P, n_heads, TOKEN_TILES, HEAD], F32)
+            heads = out_heads[first // HEAD : first // HEAD + n_heads].rearrange(
                 "h (p i) d -> p h i d", i=TOKEN_TILES
             )
             if head_gain is None:
                 for i in range(TOKEN_TILES):
                     target = stage[:, :, i, :]
-                    source = acc_tiles[(rho, i)][:].rearrange("p (h d) -> p h d", h=HEADS)
+                    source = acc_tiles[(rho, i)][:].rearrange("p (h d) -> p h d", h=n_heads)
                     if i % 2 == 0:
                         nc.scalar.copy(out=target, in_=source)
                     else:
@@ -181,19 +183,20 @@ def tile_groupedqueryattention_pa_kernel(
                     )
                 nc.sync.dma_start(out=heads, in_=stage[:])
 
-        x_raw = xpool.tile([P, TOKEN_TILES, D_MODEL], BF16)
         x_rows = x[0].rearrange("(p i) k -> p i k", i=TOKEN_TILES)
         first_k = 2 * K_PASS
-        load(0, pieces=2)
+        load(0, 0, BANK)
+        load(0, BANK, BANK)
         load(1)
-        nc.sync.dma_start(out=x_raw[:, :, 0:first_k], in_=x_rows[:, :, 0:first_k])
+        x_first = xpool.tile([P, TOKEN_TILES, first_k], BF16)
+        nc.sync.dma_start(out=x_first[:], in_=x_rows[:, :, 0:first_k])
         scale_rows = const.tile([P, 2 * HEAD], BF16)
         nc.vector.memset(scale_rows[:], 0.0)
         nc.sync.dma_start(out=scale_rows[0:1, 0:HEAD], in_=q_scale.unsqueeze(0))
         nc.sync.dma_start(out=scale_rows[0:1, HEAD:], in_=k_scale.unsqueeze(0))
-        load(2)
-        nc.sync.dma_start(out=x_raw[:, :, first_k:], in_=x_rows[:, :, first_k:])
-        for s in range(3, RAW_BUFS):
+        x_rest = xpool.tile([P, TOKEN_TILES, D_MODEL - first_k], BF16)
+        nc.sync.dma_start(out=x_rest[:], in_=x_rows[:, :, first_k:])
+        for s in range(2, RAW_BUFS[SLAB] + 1):
             load(s)
 
         ident = const.tile([P, P], F32)
@@ -209,13 +212,15 @@ def tile_groupedqueryattention_pa_kernel(
         x_scales = xpool.tile([P, PASSES, TOKENS], U8, align_bytes=64)
 
         def prepare_x(g):
+            k = g * K_PASS
+            x_raw, start = (x_first, k) if k < first_k else (x_rest, k - first_k)
             x_grouped = xg_pool.tile([P, TOKENS * PACK], BF16, align_bytes=64)
             for pair in range(TOKEN_TILES // 2):
                 xt = psum.tile([P, 2, 2 * P], F32, tag="bank")
                 for u in range(2):
                     for half in range(2):
                         i = 2 * pair + half
-                        words = x_raw[:, i, g * K_PASS : (g + 1) * K_PASS].bitcast(F32)
+                        words = x_raw[:, i, start : start + K_PASS].bitcast(F32)
                         nc.tensor.transpose(
                             xt[:, u, half * P : (half + 1) * P],
                             words.rearrange("p (q u) -> p q u", u=2)[:, :, u],
@@ -235,9 +240,12 @@ def tile_groupedqueryattention_pa_kernel(
             nc.tensor.matmul(out=spread[:], lhsT=ones[:], rhs=scale_rows[:], start=True, stop=True)
             nc.vector.tensor_scalar_add(out=gain[:], in0=spread[:], scalar1=1.0)
 
-        order = [(rho, g) for rho in range(2 * len(groups)) for g in range(PASSES)]
+        order = [(rho, g) for rho in range(len(rounds)) for g in range(PASSES)]
         done = 0
         waiting = []
+        for g in range(PASSES):
+            prepare_x(g)
+        spread_gains()
         for m in range(-REGROUP_AHEAD, len(jobs) + 2):
             if m + REGROUP_AHEAD < len(jobs):
                 regroup(m + REGROUP_AHEAD)
@@ -247,21 +255,14 @@ def tile_groupedqueryattention_pa_kernel(
                 empty(rho)
             if 0 <= m + QUANTISE_AHEAD < len(jobs):
                 quantise(m + QUANTISE_AHEAD)
-            if m == 0:
-                prepare_x(0)
-                prepare_x(1)
-                spread_gains()
-            if m == 1:
-                for g in range(2, PASSES):
-                    prepare_x(g)
-            while m >= 1 and done < len(order) and order[done] in code_tiles:
+            while m >= 0 and done < len(order):
                 rho, g = order[done]
-                s, first, width = jobs[min(m, len(jobs) - 1)]
+                c, first, width = rounds[rho]
+                if (c * PASSES + g, first) not in code_tiles:
+                    break
                 multiply(rho, g)
                 done += 1
                 if g == PASSES - 1:
-                    if groups[rho // 2][2] is not None:
+                    if groups[c][2] is not None:
                         root_mean_squares(rho)
-                        waiting.append((rho, m + 1))
-                    else:
-                        waiting.append((rho, m + 1))
+                    waiting.append((rho, m + 1))

@@ -86,16 +86,16 @@ def tile_groupedqueryattention_pa_kernel(
         def regroup(m):
             s, first, width = jobs[m]
             raw = raw_tiles[(s, first)]
-            split = width * VECTOR_SHARE // 64
+            split = width * VECTOR_SHARE // 1024 * 16
             grouped = grouped_pool.tile([P, width, PACK], BF16, align_bytes=64)
             nc.vector.tensor_copy(
-                out=grouped[:, 0:split, :].rearrange("p (c i) t -> p c t i", i=4),
-                in_=raw[:, :, 0:split].rearrange("p t (c i) -> p c t i", i=4),
+                out=grouped[:, 0:split, :].rearrange("p (c i) t -> p c t i", i=8),
+                in_=raw[:, :, 0:split].rearrange("p t (c i) -> p c t i", i=8),
             )
             nc.scalar.copy(
-                out=grouped[:, split:, :].rearrange("p (c i) t -> p c t i", i=4),
+                out=grouped[:, split:, :].rearrange("p (c i) t -> p c t i", i=8),
                 in_=raw[:, :, split:width].rearrange(
-                    "p t (c i) -> p c t i", i=4
+                    "p t (c i) -> p c t i", i=8
                 ),
             )
             grouped_tiles[m] = grouped

@@ -23,8 +23,9 @@ BANK = 512
 HEADS = BANK // HEAD
 SLAB = 2 * BANK
 EPS = 1e-6
-VECTOR_SHARE = 33
+VECTOR_SHARE = 32
 RAW_BUFS = {SLAB: 8, BANK: 2}
+PAIRED_GROUPS = 2
 REGROUP_AHEAD = 2
 QUANTISE_AHEAD = 1
 
@@ -41,7 +42,7 @@ def tile_groupedqueryattention_pa_kernel(
         xg_pool = ctx.enter_context(tc.tile_pool(name="xgrouped", bufs=2))
         raw_pool = ctx.enter_context(tc.tile_pool(name="raw", bufs=2))
         grouped_pool = ctx.enter_context(tc.tile_pool(name="grouped", bufs=4))
-        codes_pool = ctx.enter_context(tc.tile_pool(name="codes", bufs=8))
+        codes_pool = ctx.enter_context(tc.tile_pool(name="codes", bufs=9))
         stage_pool = ctx.enter_context(tc.tile_pool(name="stage", bufs=3))
         squares_pool = ctx.enter_context(tc.tile_pool(name="squares", bufs=2))
         small = ctx.enter_context(tc.tile_pool(name="small", bufs=3))
@@ -59,16 +60,16 @@ def tile_groupedqueryattention_pa_kernel(
         rounds = [(c, first, BANK) for c in range(last_group) for first in (0, BANK)]
         rounds += [(last_group, 0, BANK), (last_group, BANK, HEAD), (last_group, BANK + HEAD, HEAD)]
         jobs = [(0, 0, BANK), (0, BANK, BANK)]
-        for s in range(1, last_group * PASSES):
+        for s in range(1, PAIRED_GROUPS * PASSES):
             jobs.append((s, 0, SLAB))
-        for c, first, width in rounds[2 * last_group :]:
+        for c, first, width in rounds[2 * PAIRED_GROUPS :]:
             for g in range(PASSES):
                 jobs.append((c * PASSES + g, first, width))
         raw_tiles = {}
         grouped_tiles = {}
         code_tiles = {}
         acc_tiles = {}
-        rms_tiles = {}
+        inv_rms_tiles = {}
 
         def load(s, first=0, width=SLAB):
             w_cols = groups[s // PASSES][0]
@@ -86,18 +87,16 @@ def tile_groupedqueryattention_pa_kernel(
         def regroup(m):
             s, first, width = jobs[m]
             raw = raw_tiles[(s, first)]
-            split = width * VECTOR_SHARE // 1024 * 16
+            split = width * VECTOR_SHARE // 64
             grouped = grouped_pool.tile([P, width, PACK], BF16, align_bytes=64)
-            nc.vector.tensor_copy(
-                out=grouped[:, 0:split, :].rearrange("p (c i) t -> p c t i", i=8),
-                in_=raw[:, :, 0:split].rearrange("p t (c i) -> p c t i", i=8),
-            )
-            nc.scalar.copy(
-                out=grouped[:, split:, :].rearrange("p (c i) t -> p c t i", i=8),
-                in_=raw[:, :, split:width].rearrange(
-                    "p t (c i) -> p c t i", i=8
-                ),
-            )
+            for copy, cols in (
+                (nc.scalar.copy, slice(split, width)),
+                (nc.vector.tensor_copy, slice(0, split)),
+            ):
+                copy(
+                    out=grouped[:, cols, :].rearrange("p (c i) t -> p c t i", i=8),
+                    in_=raw[:, :, cols].rearrange("p t (c i) -> p c t i", i=8),
+                )
             grouped_tiles[m] = grouped
             if s > 0 and first + width == SLAB and s + RAW_BUFS[SLAB] < slabs:
                 load(s + RAW_BUFS[SLAB])
@@ -144,11 +143,15 @@ def tile_groupedqueryattention_pa_kernel(
                     func=ACT.Square,
                     accum_out=sumsq[:, m : m + 1],
                 )
-            rms = small.tile([P, len(pieces)], F32)
+            inv_rms = small.tile([P, len(pieces)], F32)
             nc.scalar.activation(
-                out=rms[:], in_=sumsq[:], func=ACT.Sqrt, scale=1.0 / HEAD, bias=eps[:]
+                out=inv_rms[:],
+                in_=sumsq[:],
+                func=ACT.Abs_reciprocal_sqrt,
+                scale=1.0 / HEAD,
+                bias=eps[:],
             )
-            rms_tiles[rho] = rms
+            inv_rms_tiles[rho] = inv_rms
 
         def empty(rho):
             c, first, width = rounds[rho]
@@ -162,7 +165,7 @@ def tile_groupedqueryattention_pa_kernel(
                 for i in range(TOKEN_TILES):
                     target = stage[:, :, i, :]
                     source = acc_tiles[(rho, i)][:].rearrange("p (h d) -> p h d", h=n_heads)
-                    if i % 2 == 0:
+                    if i < TOKEN_TILES - 1:
                         nc.scalar.copy(out=target, in_=source)
                     else:
                         nc.vector.tensor_copy(out=target, in_=source)
@@ -170,8 +173,7 @@ def tile_groupedqueryattention_pa_kernel(
                         two = slice(i - 1, i + 1)
                         nc.sync.dma_start(out=heads[:, :, two, :], in_=stage[:, :, two, :])
             else:
-                inv_rms = small.tile([P, len(pieces)], F32)
-                nc.vector.reciprocal(out=inv_rms[:], in_=rms_tiles[rho][:])
+                inv_rms = inv_rms_tiles[rho]
                 for m, (i, h) in enumerate(pieces):
                     nc.vector.scalar_tensor_tensor(
                         out=stage[:, h, i, :],
@@ -184,19 +186,28 @@ def tile_groupedqueryattention_pa_kernel(
                 nc.sync.dma_start(out=heads, in_=stage[:])
 
         x_rows = x[0].rearrange("(p i) k -> p i k", i=TOKEN_TILES)
-        first_k = 2 * K_PASS
+        x_tiles = {}
+
+        def load_x(first, passes):
+            tile = xpool.tile([P, TOKEN_TILES, passes * K_PASS], BF16, tag=f"x{first}")
+            cols = slice(first * K_PASS, (first + passes) * K_PASS)
+            nc.sync.dma_start(out=tile[:], in_=x_rows[:, :, cols])
+            for g in range(passes):
+                x_tiles[first + g] = tile[:, :, g * K_PASS : (g + 1) * K_PASS]
+
         load(0, 0, BANK)
         load(0, BANK, BANK)
         load(1)
-        x_first = xpool.tile([P, TOKEN_TILES, first_k], BF16)
-        nc.sync.dma_start(out=x_first[:], in_=x_rows[:, :, 0:first_k])
+        load_x(0, 2)
         scale_rows = const.tile([P, 2 * HEAD], BF16)
         nc.vector.memset(scale_rows[:], 0.0)
         nc.sync.dma_start(out=scale_rows[0:1, 0:HEAD], in_=q_scale.unsqueeze(0))
         nc.sync.dma_start(out=scale_rows[0:1, HEAD:], in_=k_scale.unsqueeze(0))
-        x_rest = xpool.tile([P, TOKEN_TILES, D_MODEL - first_k], BF16)
-        nc.sync.dma_start(out=x_rest[:], in_=x_rows[:, :, first_k:])
-        for s in range(2, RAW_BUFS[SLAB] + 1):
+        load(2)
+        load_x(2, 2)
+        load(3)
+        load_x(4, 1)
+        for s in range(4, RAW_BUFS[SLAB] + 1):
             load(s)
 
         ident = const.tile([P, P], F32)
@@ -204,23 +215,24 @@ def tile_groupedqueryattention_pa_kernel(
         eps = const.tile([P, 1], F32)
         nc.vector.memset(eps[:], EPS)
         first_sqrt = const.tile([P, 1], F32)
-        nc.scalar.activation(out=first_sqrt[:], in_=eps[:], func=ACT.Sqrt)
+        nc.scalar.activation(out=first_sqrt[:], in_=eps[:], func=ACT.Abs_reciprocal_sqrt)
         ones = const.tile([P, P], BF16)
         nc.vector.memset(ones[:], 1.0)
 
         x_codes = xpool.tile([P, PASSES, TOKENS], U32, align_bytes=64)
         x_scales = xpool.tile([P, PASSES, TOKENS], U8, align_bytes=64)
 
+        x_ready = set()
+
         def prepare_x(g):
-            k = g * K_PASS
-            x_raw, start = (x_first, k) if k < first_k else (x_rest, k - first_k)
+            x_ready.add(g)
             x_grouped = xg_pool.tile([P, TOKENS * PACK], BF16, align_bytes=64)
             for pair in range(TOKEN_TILES // 2):
                 xt = psum.tile([P, 2, 2 * P], F32, tag="bank")
                 for u in range(2):
                     for half in range(2):
                         i = 2 * pair + half
-                        words = x_raw[:, i, start : start + K_PASS].bitcast(F32)
+                        words = x_tiles[g][:, i, :].bitcast(F32)
                         nc.tensor.transpose(
                             xt[:, u, half * P : (half + 1) * P],
                             words.rearrange("p (q u) -> p q u", u=2)[:, :, u],
@@ -228,7 +240,8 @@ def tile_groupedqueryattention_pa_kernel(
                         )
                 columns = x_grouped[:, pair * 2 * P * PACK : (pair + 1) * 2 * P * PACK]
                 target = columns.bitcast(F32).rearrange("p (r u) -> p r u", u=2)
-                nc.scalar.copy(out=target, in_=xt[:].rearrange("p u r -> p r u"))
+                copy = nc.scalar.copy if pair == 0 else nc.vector.tensor_copy
+                copy(out=target, in_=xt[:].rearrange("p u r -> p r u"))
             nc.vector.quantize_mx(
                 out=x_codes[:, g, :].bitcast(FP8X4),
                 scales=x_scales[:, g, :],
@@ -242,27 +255,36 @@ def tile_groupedqueryattention_pa_kernel(
 
         order = [(rho, g) for rho in range(len(rounds)) for g in range(PASSES)]
         done = 0
-        waiting = []
-        for g in range(PASSES):
-            prepare_x(g)
-        spread_gains()
-        for m in range(-REGROUP_AHEAD, len(jobs) + 2):
-            if m + REGROUP_AHEAD < len(jobs):
-                regroup(m + REGROUP_AHEAD)
-            ready = [rho for rho, step in waiting if step <= m]
-            waiting = [(rho, step) for rho, step in waiting if step > m]
-            for rho in ready:
-                empty(rho)
-            if 0 <= m + QUANTISE_AHEAD < len(jobs):
-                quantise(m + QUANTISE_AHEAD)
-            while m >= 0 and done < len(order):
-                rho, g = order[done]
-                c, first, width = rounds[rho]
-                if (c * PASSES + g, first) not in code_tiles:
-                    break
-                multiply(rho, g)
-                done += 1
-                if g == PASSES - 1:
-                    if groups[c][2] is not None:
-                        root_mean_squares(rho)
-                    waiting.append((rho, m + 1))
+        later = {}
+        with tc.manual_schedule(
+            engines={
+                mybir.EngineType.PE,
+                mybir.EngineType.Activation,
+                mybir.EngineType.DVE,
+            }
+        ):
+            for m in range(-REGROUP_AHEAD, len(jobs) + 8):
+                for g in {1: (0, 1), 3: (2, 3, 4)}.get(m, ()):
+                    prepare_x(g)
+                if m == 3:
+                    spread_gains()
+                if m + REGROUP_AHEAD < len(jobs):
+                    regroup(m + REGROUP_AHEAD)
+                for step, rho in later.get(m, ()):
+                    step(rho)
+                if 0 <= m + QUANTISE_AHEAD < len(jobs):
+                    quantise(m + QUANTISE_AHEAD)
+                while done < len(order):
+                    rho, g = order[done]
+                    c, first, width = rounds[rho]
+                    if (c * PASSES + g, first) not in code_tiles or g not in x_ready:
+                        break
+                    multiply(rho, g)
+                    done += 1
+                    if g == PASSES - 1:
+                        if groups[c][2] is None:
+                            later.setdefault(m + 3, []).append((empty, rho))
+                        else:
+                            n = m + 3 + rho % 2
+                            later.setdefault(n, []).append((root_mean_squares, rho))
+                            later.setdefault(n + 2, []).append((empty, rho))

@@ -23,9 +23,10 @@ BANK = 512
 HEADS = BANK // HEAD
 SLAB = 2 * BANK
 EPS = 1e-6
-VECTOR_SHARE = 32
-RAW_BUFS = {SLAB: 8, BANK: 2}
-PAIRED_GROUPS = 2
+VECTOR_SHARE = 33
+RAW_BUFS = 9
+TRAIL = 2
+PAIRED_GROUPS = 3
 REGROUP_AHEAD = 2
 QUANTISE_AHEAD = 1
 
@@ -39,11 +40,11 @@ def tile_groupedqueryattention_pa_kernel(
     with ExitStack() as ctx:
         const = ctx.enter_context(tc.tile_pool(name="const", bufs=1))
         xpool = ctx.enter_context(tc.tile_pool(name="xpool", bufs=1))
-        xg_pool = ctx.enter_context(tc.tile_pool(name="xgrouped", bufs=2))
-        raw_pool = ctx.enter_context(tc.tile_pool(name="raw", bufs=2))
+        xg_pool = ctx.enter_context(tc.tile_pool(name="xgrouped", bufs=3))
+        raw_pool = ctx.enter_context(tc.tile_pool(name="raw", bufs=RAW_BUFS))
         grouped_pool = ctx.enter_context(tc.tile_pool(name="grouped", bufs=4))
         codes_pool = ctx.enter_context(tc.tile_pool(name="codes", bufs=9))
-        stage_pool = ctx.enter_context(tc.tile_pool(name="stage", bufs=3))
+        stage_pool = ctx.enter_context(tc.tile_pool(name="stage", bufs=4))
         squares_pool = ctx.enter_context(tc.tile_pool(name="squares", bufs=2))
         small = ctx.enter_context(tc.tile_pool(name="small", bufs=3))
         psum = ctx.enter_context(tc.psum_pool(name="psum", bufs=8))
@@ -71,23 +72,20 @@ def tile_groupedqueryattention_pa_kernel(
         acc_tiles = {}
         inv_rms_tiles = {}
 
-        def load(s, first=0, width=SLAB):
+        def load(s):
             w_cols = groups[s // PASSES][0]
             g = s % PASSES
-            raw = raw_pool.tile([P, PACK, width], BF16, tag=f"raw{width}", bufs=RAW_BUFS[width])
+            raw = raw_pool.tile([P, PACK, SLAB], BF16)
             nc.sync.dma_start(
                 out=raw[:],
-                in_=w_cols[g * K_PASS : (g + 1) * K_PASS, first : first + width].rearrange(
-                    "(p t) c -> p t c", t=PACK
-                ),
+                in_=w_cols[g * K_PASS : (g + 1) * K_PASS, :].rearrange("(p t) c -> p t c", t=PACK),
             )
-            for c in range(first, first + width, HEAD):
-                raw_tiles[(s, c)] = raw[:, :, c - first :]
+            raw_tiles[s] = raw
 
         def regroup(m):
             s, first, width = jobs[m]
-            raw = raw_tiles[(s, first)]
-            split = width * VECTOR_SHARE // 64
+            raw = raw_tiles[s]
+            split = width * VECTOR_SHARE // 1024 * 16
             grouped = grouped_pool.tile([P, width, PACK], BF16, align_bytes=64)
             for copy, cols in (
                 (nc.scalar.copy, slice(split, width)),
@@ -95,11 +93,13 @@ def tile_groupedqueryattention_pa_kernel(
             ):
                 copy(
                     out=grouped[:, cols, :].rearrange("p (c i) t -> p c t i", i=8),
-                    in_=raw[:, :, cols].rearrange("p t (c i) -> p c t i", i=8),
+                    in_=raw[:, :, first + cols.start : first + cols.stop].rearrange(
+                        "p t (c i) -> p c t i", i=8
+                    ),
                 )
             grouped_tiles[m] = grouped
-            if s > 0 and first + width == SLAB and s + RAW_BUFS[SLAB] < slabs:
-                load(s + RAW_BUFS[SLAB])
+            if first + width == SLAB and s + RAW_BUFS < slabs:
+                load(s + RAW_BUFS)
 
         def quantise(m):
             s, first, width = jobs[m]
@@ -188,26 +188,21 @@ def tile_groupedqueryattention_pa_kernel(
         x_rows = x[0].rearrange("(p i) k -> p i k", i=TOKEN_TILES)
         x_tiles = {}
 
-        def load_x(first, passes):
-            tile = xpool.tile([P, TOKEN_TILES, passes * K_PASS], BF16, tag=f"x{first}")
-            cols = slice(first * K_PASS, (first + passes) * K_PASS)
-            nc.sync.dma_start(out=tile[:], in_=x_rows[:, :, cols])
-            for g in range(passes):
-                x_tiles[first + g] = tile[:, :, g * K_PASS : (g + 1) * K_PASS]
+        def load_x(pair):
+            tile = xpool.tile([P, 2, D_MODEL], BF16, tag=f"x{pair}")
+            nc.sync.dma_start(out=tile[:], in_=x_rows[:, 2 * pair : 2 * pair + 2, :])
+            x_tiles[pair] = tile
 
-        load(0, 0, BANK)
-        load(0, BANK, BANK)
+        load(0)
         load(1)
-        load_x(0, 2)
+        load_x(0)
         scale_rows = const.tile([P, 2 * HEAD], BF16)
         nc.vector.memset(scale_rows[:], 0.0)
         nc.sync.dma_start(out=scale_rows[0:1, 0:HEAD], in_=q_scale.unsqueeze(0))
         nc.sync.dma_start(out=scale_rows[0:1, HEAD:], in_=k_scale.unsqueeze(0))
         load(2)
-        load_x(2, 2)
-        load(3)
-        load_x(4, 1)
-        for s in range(4, RAW_BUFS[SLAB] + 1):
+        load_x(1)
+        for s in range(3, RAW_BUFS):
             load(s)
 
         ident = const.tile([P, P], F32)
@@ -222,38 +217,40 @@ def tile_groupedqueryattention_pa_kernel(
         x_codes = xpool.tile([P, PASSES, TOKENS], U32, align_bytes=64)
         x_scales = xpool.tile([P, PASSES, TOKENS], U8, align_bytes=64)
 
-        x_ready = set()
-
-        def prepare_x(g):
-            x_ready.add(g)
-            x_grouped = xg_pool.tile([P, TOKENS * PACK], BF16, align_bytes=64)
-            for pair in range(TOKEN_TILES // 2):
+        def prepare_x(pair):
+            for g in range(PASSES):
                 xt = psum.tile([P, 2, 2 * P], F32, tag="bank")
                 for u in range(2):
                     for half in range(2):
-                        i = 2 * pair + half
-                        words = x_tiles[g][:, i, :].bitcast(F32)
+                        words = x_tiles[pair][:, half, g * K_PASS : (g + 1) * K_PASS].bitcast(F32)
                         nc.tensor.transpose(
                             xt[:, u, half * P : (half + 1) * P],
                             words.rearrange("p (q u) -> p q u", u=2)[:, :, u],
                             ident[:],
                         )
-                columns = x_grouped[:, pair * 2 * P * PACK : (pair + 1) * 2 * P * PACK]
-                target = columns.bitcast(F32).rearrange("p (r u) -> p r u", u=2)
-                copy = nc.scalar.copy if pair == 0 else nc.vector.tensor_copy
-                copy(out=target, in_=xt[:].rearrange("p u r -> p r u"))
-            nc.vector.quantize_mx(
-                out=x_codes[:, g, :].bitcast(FP8X4),
-                scales=x_scales[:, g, :],
-                in_=x_grouped[:],
-            )
+                x_grouped = xg_pool.tile([P, 2 * P * PACK], BF16, align_bytes=64)
+                nc.scalar.copy(
+                    out=x_grouped[:].bitcast(F32).rearrange("p (r u) -> p r u", u=2),
+                    in_=xt[:].rearrange("p u r -> p r u"),
+                )
+                tokens = slice(pair * 2 * P, (pair + 1) * 2 * P)
+                nc.vector.quantize_mx(
+                    out=x_codes[:, g, tokens].bitcast(FP8X4),
+                    scales=x_scales[:, g, tokens],
+                    in_=x_grouped[:],
+                )
 
         def spread_gains():
             spread = psum.tile([P, BANK], F32, tag="bank")
             nc.tensor.matmul(out=spread[:], lhsT=ones[:], rhs=scale_rows[:], start=True, stop=True)
             nc.vector.tensor_scalar_add(out=gain[:], in0=spread[:], scalar1=1.0)
 
-        order = [(rho, g) for rho in range(len(rounds)) for g in range(PASSES)]
+        order = []
+        for c in range(PAIRED_GROUPS):
+            for g in range(PASSES + TRAIL):
+                order.extend([(2 * c, g)] if g < PASSES else [])
+                order.extend([(2 * c + 1, g - TRAIL)] if g >= TRAIL else [])
+        order.extend((rho, g) for rho in range(2 * PAIRED_GROUPS, len(rounds)) for g in range(PASSES))
         done = 0
         later = {}
         with tc.manual_schedule(
@@ -264,9 +261,9 @@ def tile_groupedqueryattention_pa_kernel(
             }
         ):
             for m in range(-REGROUP_AHEAD, len(jobs) + 8):
-                for g in {1: (0, 1), 3: (2, 3, 4)}.get(m, ()):
-                    prepare_x(g)
-                if m == 3:
+                if m in (1, 2):
+                    prepare_x(m - 1)
+                if m == 2:
                     spread_gains()
                 if m + REGROUP_AHEAD < len(jobs):
                     regroup(m + REGROUP_AHEAD)
@@ -274,10 +271,10 @@ def tile_groupedqueryattention_pa_kernel(
                     step(rho)
                 if 0 <= m + QUANTISE_AHEAD < len(jobs):
                     quantise(m + QUANTISE_AHEAD)
-                while done < len(order):
+                while m >= 2 and done < len(order):
                     rho, g = order[done]
                     c, first, width = rounds[rho]
-                    if (c * PASSES + g, first) not in code_tiles or g not in x_ready:
+                    if (c * PASSES + g, first) not in code_tiles:
                         break
                     multiply(rho, g)
                     done += 1
@@ -285,6 +282,5 @@ def tile_groupedqueryattention_pa_kernel(
                         if groups[c][2] is None:
                             later.setdefault(m + 3, []).append((empty, rho))
                         else:
-                            n = m + 3 + rho % 2
-                            later.setdefault(n, []).append((root_mean_squares, rho))
-                            later.setdefault(n + 2, []).append((empty, rho))
+                            later.setdefault(m + 2, []).append((root_mean_squares, rho))
+                            later.setdefault(m + 4, []).append((empty, rho))

@@ -25,7 +25,7 @@ SLAB = 2 * BANK
 EPS = 1e-6
 VECTOR_SHARE = 33
 RAW_BUFS = 9
-TRAIL = 2
+TRAIL = 3
 PAIRED_GROUPS = 3
 REGROUP_AHEAD = 2
 QUANTISE_AHEAD = 1
@@ -165,7 +165,8 @@ def tile_groupedqueryattention_pa_kernel(
                 for i in range(TOKEN_TILES):
                     target = stage[:, :, i, :]
                     source = acc_tiles[(rho, i)][:].rearrange("p (h d) -> p h d", h=n_heads)
-                    if i < TOKEN_TILES - 1:
+                    on_scalar = i % 2 == 0 if rho == len(rounds) - 1 else i < TOKEN_TILES - 1
+                    if on_scalar:
                         nc.scalar.copy(out=target, in_=source)
                     else:
                         nc.vector.tensor_copy(out=target, in_=source)
@@ -280,7 +281,8 @@ def tile_groupedqueryattention_pa_kernel(
                     done += 1
                     if g == PASSES - 1:
                         if groups[c][2] is None:
-                            later.setdefault(m + 3, []).append((empty, rho))
+                            later.setdefault(m + 5, []).append((empty, rho))
                         else:
-                            later.setdefault(m + 2, []).append((root_mean_squares, rho))
-                            later.setdefault(m + 4, []).append((empty, rho))
+                            n = m + 2 + rho % 2
+                            later.setdefault(n, []).append((root_mean_squares, rho))
+                            later.setdefault(n + 2, []).append((empty, rho))

@@ -23,9 +23,10 @@ BANK = 512
 HEADS = BANK // HEAD
 SLAB = 2 * BANK
 EPS = 1e-6
-VECTOR_SHARE = 33
+VECTOR_SHARE = 31
 RAW_BUFS = 9
 TRAIL = 3
+GPSIMD_SHARE = 16
 PAIRED_GROUPS = 3
 REGROUP_AHEAD = 2
 QUANTISE_AHEAD = 1
@@ -82,13 +83,14 @@ def tile_groupedqueryattention_pa_kernel(
             )
             raw_tiles[s] = raw
 
-        def regroup(m):
+        def regroup(m, gpsimd_share):
             s, first, width = jobs[m]
             raw = raw_tiles[s]
             split = width * VECTOR_SHARE // 1024 * 16
+            end = width - width * gpsimd_share // 64
             grouped = grouped_pool.tile([P, width, PACK], BF16, align_bytes=64)
             for copy, cols in (
-                (nc.scalar.copy, slice(split, width)),
+                (nc.scalar.copy, slice(split, end)),
                 (nc.vector.tensor_copy, slice(0, split)),
             ):
                 copy(
@@ -98,8 +100,18 @@ def tile_groupedqueryattention_pa_kernel(
                     ),
                 )
             grouped_tiles[m] = grouped
-            if first + width == SLAB and s + RAW_BUFS < slabs:
-                load(s + RAW_BUFS)
+
+        def regroup_rest(m, gpsimd_share, ready):
+            s, first, width = jobs[m]
+            start = width - width * gpsimd_share // 64
+            nc.gpsimd.tensor_scalar(
+                out=grouped_tiles[m][:, start:, :],
+                in0=raw_tiles[s][:, :, first + start : first + width].rearrange("p t c -> p c t"),
+                scalar1=ready[:, 0:1],
+                scalar2=0.0,
+                op0=ALU.mult,
+                op1=ALU.add,
+            )
 
         def quantise(m):
             s, first, width = jobs[m]
@@ -153,7 +165,7 @@ def tile_groupedqueryattention_pa_kernel(
             )
             inv_rms_tiles[rho] = inv_rms
 
-        def empty(rho):
+        def empty(rho, job=None):
             c, first, width = rounds[rho]
             w_cols, out_heads, head_gain = groups[c]
             n_heads = width // HEAD
@@ -175,6 +187,17 @@ def tile_groupedqueryattention_pa_kernel(
                         nc.sync.dma_start(out=heads[:, :, two, :], in_=stage[:, :, two, :])
             else:
                 inv_rms = inv_rms_tiles[rho]
+                if job is not None:
+                    ready = small.tile([P, 1], F32)
+                    nc.vector.tensor_scalar(
+                        out=ready[:],
+                        in0=inv_rms[:, 0:1],
+                        scalar1=0.0,
+                        scalar2=1.0,
+                        op0=ALU.mult,
+                        op1=ALU.add,
+                    )
+                    regroup_rest(job, GPSIMD_SHARE, ready)
                 for m, (i, h) in enumerate(pieces):
                     nc.vector.scalar_tensor_tensor(
                         out=stage[:, h, i, :],
@@ -266,10 +289,19 @@ def tile_groupedqueryattention_pa_kernel(
                     prepare_x(m - 1)
                 if m == 2:
                     spread_gains()
-                if m + REGROUP_AHEAD < len(jobs):
-                    regroup(m + REGROUP_AHEAD)
+                job = m + REGROUP_AHEAD
+                norms = [rho for step, rho in later.get(m, ()) if step is empty and rho in inv_rms_tiles]
+                if job < len(jobs):
+                    regroup(job, GPSIMD_SHARE if norms else 0)
                 for step, rho in later.get(m, ()):
-                    step(rho)
+                    if rho in norms and step is empty:
+                        step(rho, job)
+                    else:
+                        step(rho)
+                if job < len(jobs):
+                    s, first, width = jobs[job]
+                    if first + width == SLAB and s + RAW_BUFS < slabs:
+                        load(s + RAW_BUFS)
                 if 0 <= m + QUANTISE_AHEAD < len(jobs):
                     quantise(m + QUANTISE_AHEAD)
                 while m >= 2 and done < len(order):

@@ -23,7 +23,7 @@ BANK = 512
 HEADS = BANK // HEAD
 SLAB = 2 * BANK
 EPS = 1e-6
-VECTOR_SHARE = 31
+VECTOR_SHARE = 30
 RAW_BUFS = 9
 TRAIL = 3
 GPSIMD_SHARE = 16

@@ -23,10 +23,10 @@ BANK = 512
 HEADS = BANK // HEAD
 SLAB = 2 * BANK
 EPS = 1e-6
-VECTOR_SHARE = 30
+VECTOR_SHARES = (36, 29, 29, 32)
 RAW_BUFS = 9
 TRAIL = 3
-GPSIMD_SHARE = 16
+GPSIMD_SHARE = 24
 PAIRED_GROUPS = 3
 REGROUP_AHEAD = 2
 QUANTISE_AHEAD = 1
@@ -86,7 +86,7 @@ def tile_groupedqueryattention_pa_kernel(
         def regroup(m, gpsimd_share):
             s, first, width = jobs[m]
             raw = raw_tiles[s]
-            split = width * VECTOR_SHARE // 1024 * 16
+            split = width * VECTOR_SHARES[s // PASSES] // 1024 * 16
             end = width - width * gpsimd_share // 64
             grouped = grouped_pool.tile([P, width, PACK], BF16, align_bytes=64)
             for copy, cols in (
@@ -315,6 +315,6 @@ def tile_groupedqueryattention_pa_kernel(
                         if groups[c][2] is None:
                             later.setdefault(m + 5, []).append((empty, rho))
                         else:
-                            n = m + 2 + rho % 2
+                            n = m + 2 + rho % 2 + (1 if c == PAIRED_GROUPS - 1 else 0)
                             later.setdefault(n, []).append((root_mean_squares, rho))
                             later.setdefault(n + 2, []).append((empty, rho))

@@ -23,10 +23,11 @@ BANK = 512
 HEADS = BANK // HEAD
 SLAB = 2 * BANK
 EPS = 1e-6
-VECTOR_SHARES = (36, 29, 29, 32)
-RAW_BUFS = 9
+VECTOR_SHARES = (36, 30, 30, 30)
+RAW_BUFS = 8
 TRAIL = 3
-GPSIMD_SHARE = 24
+GPSIMD_SHARE = 28
+VECTOR_SHARE_BESIDE_NORM = 18
 PAIRED_GROUPS = 3
 REGROUP_AHEAD = 2
 QUANTISE_AHEAD = 1
@@ -43,7 +44,7 @@ def tile_groupedqueryattention_pa_kernel(
         xpool = ctx.enter_context(tc.tile_pool(name="xpool", bufs=1))
         xg_pool = ctx.enter_context(tc.tile_pool(name="xgrouped", bufs=3))
         raw_pool = ctx.enter_context(tc.tile_pool(name="raw", bufs=RAW_BUFS))
-        grouped_pool = ctx.enter_context(tc.tile_pool(name="grouped", bufs=4))
+        grouped_pool = ctx.enter_context(tc.tile_pool(name="grouped", bufs=5))
         codes_pool = ctx.enter_context(tc.tile_pool(name="codes", bufs=9))
         stage_pool = ctx.enter_context(tc.tile_pool(name="stage", bufs=4))
         squares_pool = ctx.enter_context(tc.tile_pool(name="squares", bufs=2))
@@ -86,7 +87,8 @@ def tile_groupedqueryattention_pa_kernel(
         def regroup(m, gpsimd_share):
             s, first, width = jobs[m]
             raw = raw_tiles[s]
-            split = width * VECTOR_SHARES[s // PASSES] // 1024 * 16
+            share = VECTOR_SHARE_BESIDE_NORM if gpsimd_share else VECTOR_SHARES[s // PASSES]
+            split = width * share // 1024 * 16
             end = width - width * gpsimd_share // 64
             grouped = grouped_pool.tile([P, width, PACK], BF16, align_bytes=64)
             for copy, cols in (
@@ -219,14 +221,15 @@ def tile_groupedqueryattention_pa_kernel(
 
         load(0)
         load(1)
+        load(2)
         load_x(0)
         scale_rows = const.tile([P, 2 * HEAD], BF16)
         nc.vector.memset(scale_rows[:], 0.0)
         nc.sync.dma_start(out=scale_rows[0:1, 0:HEAD], in_=q_scale.unsqueeze(0))
         nc.sync.dma_start(out=scale_rows[0:1, HEAD:], in_=k_scale.unsqueeze(0))
-        load(2)
+        load(3)
         load_x(1)
-        for s in range(3, RAW_BUFS):
+        for s in range(4, RAW_BUFS):
             load(s)
 
         ident = const.tile([P, P], F32)
@@ -285,9 +288,9 @@ def tile_groupedqueryattention_pa_kernel(
             }
         ):
             for m in range(-REGROUP_AHEAD, len(jobs) + 8):
-                if m in (1, 2):
-                    prepare_x(m - 1)
-                if m == 2:
+                if m in (2, 3):
+                    prepare_x(m - 2)
+                if m == 3:
                     spread_gains()
                 job = m + REGROUP_AHEAD
                 norms = [rho for step, rho in later.get(m, ()) if step is empty and rho in inv_rms_tiles]
@@ -304,7 +307,7 @@ def tile_groupedqueryattention_pa_kernel(
                         load(s + RAW_BUFS)
                 if 0 <= m + QUANTISE_AHEAD < len(jobs):
                     quantise(m + QUANTISE_AHEAD)
-                while m >= 2 and done < len(order):
+                while m >= 3 and done < len(order):
                     rho, g = order[done]
                     c, first, width = rounds[rho]
                     if (c * PASSES + g, first) not in code_tiles:
@@ -315,6 +318,6 @@ def tile_groupedqueryattention_pa_kernel(
                         if groups[c][2] is None:
                             later.setdefault(m + 5, []).append((empty, rho))
                         else:
-                            n = m + 2 + rho % 2 + (1 if c == PAIRED_GROUPS - 1 else 0)
+                            n = m + 1 + rho % 2 + (2 if c == PAIRED_GROUPS - 1 else 0)
                             later.setdefault(n, []).append((root_mean_squares, rho))
                             later.setdefault(n + 2, []).append((empty, rho))

@@ -26,8 +26,8 @@ EPS = 1e-6
 VECTOR_SHARES = (36, 30, 30, 30)
 RAW_BUFS = 8
 TRAIL = 3
-GPSIMD_SHARE = 28
-VECTOR_SHARE_BESIDE_NORM = 18
+GPSIMD_SHARE = 16
+VECTOR_SHARE_BESIDE_NORM = 27
 PAIRED_GROUPS = 3
 REGROUP_AHEAD = 2
 QUANTISE_AHEAD = 1

@@ -23,11 +23,11 @@ BANK = 512
 HEADS = BANK // HEAD
 SLAB = 2 * BANK
 EPS = 1e-6
-VECTOR_SHARES = (36, 30, 30, 30)
+VECTOR_SHARES = (38, 31, 31, 30)
 RAW_BUFS = 8
-TRAIL = 3
-GPSIMD_SHARE = 16
-VECTOR_SHARE_BESIDE_NORM = 27
+TRAIL = 4
+GPSIMD_SHARE = 20
+VECTOR_SHARE_BESIDE_NORM = 25
 PAIRED_GROUPS = 3
 REGROUP_AHEAD = 2
 QUANTISE_AHEAD = 1
@@ -222,14 +222,15 @@ def tile_groupedqueryattention_pa_kernel(
         load(0)
         load(1)
         load(2)
+        load(3)
         load_x(0)
         scale_rows = const.tile([P, 2 * HEAD], BF16)
         nc.vector.memset(scale_rows[:], 0.0)
         nc.sync.dma_start(out=scale_rows[0:1, 0:HEAD], in_=q_scale.unsqueeze(0))
         nc.sync.dma_start(out=scale_rows[0:1, HEAD:], in_=k_scale.unsqueeze(0))
-        load(3)
+        load(4)
         load_x(1)
-        for s in range(4, RAW_BUFS):
+        for s in range(5, RAW_BUFS):
             load(s)
 
         ident = const.tile([P, P], F32)
@@ -288,9 +289,9 @@ def tile_groupedqueryattention_pa_kernel(
             }
         ):
             for m in range(-REGROUP_AHEAD, len(jobs) + 8):
-                if m in (2, 3):
-                    prepare_x(m - 2)
-                if m == 3:
+                if m in (3, 4):
+                    prepare_x(m - 3)
+                if m == 4:
                     spread_gains()
                 job = m + REGROUP_AHEAD
                 norms = [rho for step, rho in later.get(m, ()) if step is empty and rho in inv_rms_tiles]
@@ -307,7 +308,7 @@ def tile_groupedqueryattention_pa_kernel(
                         load(s + RAW_BUFS)
                 if 0 <= m + QUANTISE_AHEAD < len(jobs):
                     quantise(m + QUANTISE_AHEAD)
-                while m >= 3 and done < len(order):
+                while m >= 4 and done < len(order):
                     rho, g = order[done]
                     c, first, width = rounds[rho]
                     if (c * PASSES + g, first) not in code_tiles:
@@ -318,6 +319,6 @@ def tile_groupedqueryattention_pa_kernel(
                         if groups[c][2] is None:
                             later.setdefault(m + 5, []).append((empty, rho))
                         else:
-                            n = m + 1 + rho % 2 + (2 if c == PAIRED_GROUPS - 1 else 0)
+                            n = m + 2 + 2 * (rho % 2)
                             later.setdefault(n, []).append((root_mean_squares, rho))
                             later.setdefault(n + 2, []).append((empty, rho))

@@ -23,11 +23,11 @@ BANK = 512
 HEADS = BANK // HEAD
 SLAB = 2 * BANK
 EPS = 1e-6
-VECTOR_SHARES = (38, 31, 31, 30)
+VECTOR_SHARES = (36, 30, 30, 32)
 RAW_BUFS = 8
 TRAIL = 4
-GPSIMD_SHARE = 20
-VECTOR_SHARE_BESIDE_NORM = 25
+GPSIMD_SHARE = 22
+VECTOR_SHARE_BESIDE_NORM = 22
 PAIRED_GROUPS = 3
 REGROUP_AHEAD = 2
 QUANTISE_AHEAD = 1
@@ -319,6 +319,6 @@ def tile_groupedqueryattention_pa_kernel(
                         if groups[c][2] is None:
                             later.setdefault(m + 5, []).append((empty, rho))
                         else:
-                            n = m + 2 + 2 * (rho % 2)
+                            n = m + 1 + 3 * (rho % 2) + (1 if c == 0 else 0)
                             later.setdefault(n, []).append((root_mean_squares, rho))
                             later.setdefault(n + 2, []).append((empty, rho))

@@ -107,8 +107,10 @@ def tile_groupedqueryattention_pa_kernel(
             s, first, width = jobs[m]
             start = width - width * gpsimd_share // 64
             nc.gpsimd.tensor_scalar(
-                out=grouped_tiles[m][:, start:, :],
-                in0=raw_tiles[s][:, :, first + start : first + width].rearrange("p t c -> p c t"),
+                out=grouped_tiles[m][:, start:, :].rearrange("p (c i) t -> p c t i", i=8),
+                in0=raw_tiles[s][:, :, first + start : first + width].rearrange(
+                    "p t (c i) -> p c t i", i=8
+                ),
                 scalar1=ready[:, 0:1],
                 scalar2=0.0,
                 op0=ALU.mult,

from contextlib import ExitStack

import concourse.mybir as mybir
from concourse.masks import make_identity

F32 = mybir.dt.float32
BF16 = mybir.dt.bfloat16
U32 = mybir.dt.uint32
U8 = mybir.dt.uint8
FP8X4 = mybir.dt.float8_e4m3fn_x4
ACT = mybir.ActivationFunctionType
ALU = mybir.AluOpType

P = 128
PACK = 4
K_PASS = P * PACK
TOKENS = 512
TOKEN_TILES = TOKENS // P
D_MODEL = 2560
PASSES = D_MODEL // K_PASS
HEAD = 256
BANK = 512
HEADS = BANK // HEAD
SLAB = 2 * BANK
EPS = 1e-6
VECTOR_SHARES = (36, 30, 30, 32)
RAW_BUFS = 8
TRAIL = 4
GPSIMD_SHARE = 22
VECTOR_SHARE_BESIDE_NORM = 22
PAIRED_GROUPS = 3
REGROUP_AHEAD = 2
QUANTISE_AHEAD = 1

FLOPS = 2 * TOKENS * D_MODEL * 4096


def tile_groupedqueryattention_pa_kernel(
    tc, x, Wq, Wk, Wv, q_scale, k_scale, out_0, out_1, out_2
):
    nc = tc.nc
    with ExitStack() as ctx:
        const = ctx.enter_context(tc.tile_pool(name="const", bufs=1))
        xpool = ctx.enter_context(tc.tile_pool(name="xpool", bufs=1))
        xg_pool = ctx.enter_context(tc.tile_pool(name="xgrouped", bufs=3))
        raw_pool = ctx.enter_context(tc.tile_pool(name="raw", bufs=RAW_BUFS))
        grouped_pool = ctx.enter_context(tc.tile_pool(name="grouped", bufs=5))
        codes_pool = ctx.enter_context(tc.tile_pool(name="codes", bufs=9))
        stage_pool = ctx.enter_context(tc.tile_pool(name="stage", bufs=4))
        squares_pool = ctx.enter_context(tc.tile_pool(name="squares", bufs=2))
        small = ctx.enter_context(tc.tile_pool(name="small", bufs=3))
        psum = ctx.enter_context(tc.psum_pool(name="psum", bufs=8))

        gain = const.tile([P, 2 * HEAD], F32)
        groups = [
            (Wk, out_1[0], gain[:, HEAD:]),
            (Wq[:, 0:SLAB], out_0[0, 0:4], gain[:, 0:HEAD]),
            (Wq[:, SLAB : 2 * SLAB], out_0[0, 4:8], gain[:, 0:HEAD]),
            (Wv, out_2[0], None),
        ]
        last_group = len(groups) - 1
        slabs = len(groups) * PASSES
        rounds = [(c, first, BANK) for c in range(last_group) for first in (0, BANK)]
        rounds += [(last_group, 0, BANK), (last_group, BANK, HEAD), (last_group, BANK + HEAD, HEAD)]
        jobs = [(0, 0, BANK), (0, BANK, BANK)]
        for s in range(1, PAIRED_GROUPS * PASSES):
            jobs.append((s, 0, SLAB))
        for c, first, width in rounds[2 * PAIRED_GROUPS :]:
            for g in range(PASSES):
                jobs.append((c * PASSES + g, first, width))
        raw_tiles = {}
        grouped_tiles = {}
        code_tiles = {}
        acc_tiles = {}
        inv_rms_tiles = {}

        def load(s):
            w_cols = groups[s // PASSES][0]
            g = s % PASSES
            raw = raw_pool.tile([P, PACK, SLAB], BF16)
            nc.sync.dma_start(
                out=raw[:],
                in_=w_cols[g * K_PASS : (g + 1) * K_PASS, :].rearrange("(p t) c -> p t c", t=PACK),
            )
            raw_tiles[s] = raw

        def regroup(m, gpsimd_share):
            s, first, width = jobs[m]
            raw = raw_tiles[s]
            share = VECTOR_SHARE_BESIDE_NORM if gpsimd_share else VECTOR_SHARES[s // PASSES]
            split = width * share // 1024 * 16
            end = width - width * gpsimd_share // 64
            grouped = grouped_pool.tile([P, width, PACK], BF16, align_bytes=64)
            for copy, cols in (
                (nc.scalar.copy, slice(split, end)),
                (nc.vector.tensor_copy, slice(0, split)),
            ):
                copy(
                    out=grouped[:, cols, :].rearrange("p (c i) t -> p c t i", i=8),
                    in_=raw[:, :, first + cols.start : first + cols.stop].rearrange(
                        "p t (c i) -> p c t i", i=8
                    ),
                )
            grouped_tiles[m] = grouped

        def regroup_rest(m, gpsimd_share, ready):
            s, first, width = jobs[m]
            start = width - width * gpsimd_share // 64
            nc.gpsimd.tensor_scalar(
                out=grouped_tiles[m][:, start:, :].rearrange("p (c i) t -> p c t i", i=8),
                in0=raw_tiles[s][:, :, first + start : first + width].rearrange(
                    "p t (c i) -> p c t i", i=8
                ),
                scalar1=ready[:, 0:1],
                scalar2=0.0,
                op0=ALU.mult,
                op1=ALU.add,
            )

        def quantise(m):
            s, first, width = jobs[m]
            codes = codes_pool.tile([P, width], U32, align_bytes=64)
            scales = codes_pool.tile([P, width], U8, align_bytes=64)
            nc.vector.quantize_mx(
                out=codes[:].bitcast(FP8X4),
                scales=scales[:],
                in_=grouped_tiles[m][:].rearrange("p c t -> p (c t)"),
            )
            for c in range(0, width, HEAD):
                code_tiles[(s, first + c)] = (codes[:, c:], scales[:, c:])

        def multiply(rho, g):
            c, first, width = rounds[rho]
            codes, scales = code_tiles[(c * PASSES + g, first)]
            for i in range(TOKEN_TILES):
                if g == 0:
                    acc = psum.tile([P, width], F32, tag="bank")
                    acc_tiles[(rho, i)] = acc
                tokens = slice(i * P, (i + 1) * P)
                nc.tensor.matmul_mx(
                    out=acc_tiles[(rho, i)][:],
                    lhsT=x_codes[:, g, tokens].bitcast(FP8X4),
                    lhsT_scale=x_scales[:, g, tokens],
                    rhs=codes[:, 0:width].bitcast(FP8X4),
                    rhs_scale=scales[:, 0:width],
                    start=(g == 0),
                    stop=(g == PASSES - 1),
                )

        pieces = [(i, h) for i in range(TOKEN_TILES) for h in range(HEADS)]

        def root_mean_squares(rho):
            sumsq = small.tile([P, len(pieces)], F32)
            for m, (i, h) in enumerate(pieces):
                squares = squares_pool.tile([P, HEAD], BF16)
                nc.scalar.activation(
                    out=squares[:],
                    in_=acc_tiles[(rho, i)][:, h * HEAD : (h + 1) * HEAD],
                    func=ACT.Square,
                    accum_out=sumsq[:, m : m + 1],
                )
            inv_rms = small.tile([P, len(pieces)], F32)
            nc.scalar.activation(
                out=inv_rms[:],
                in_=sumsq[:],
                func=ACT.Abs_reciprocal_sqrt,
                scale=1.0 / HEAD,
                bias=eps[:],
            )
            inv_rms_tiles[rho] = inv_rms

        def empty(rho, job=None):
            c, first, width = rounds[rho]
            w_cols, out_heads, head_gain = groups[c]
            n_heads = width // HEAD
            stage = stage_pool.tile([P, n_heads, TOKEN_TILES, HEAD], F32)
            heads = out_heads[first // HEAD : first // HEAD + n_heads].rearrange(
                "h (p i) d -> p h i d", i=TOKEN_TILES
            )
            if head_gain is None:
                for i in range(TOKEN_TILES):
                    target = stage[:, :, i, :]
                    source = acc_tiles[(rho, i)][:].rearrange("p (h d) -> p h d", h=n_heads)
                    on_scalar = i % 2 == 0 if rho == len(rounds) - 1 else i < TOKEN_TILES - 1
                    if on_scalar:
                        nc.scalar.copy(out=target, in_=source)
                    else:
                        nc.vector.tensor_copy(out=target, in_=source)
                    if i % 2 == 1:
                        two = slice(i - 1, i + 1)
                        nc.sync.dma_start(out=heads[:, :, two, :], in_=stage[:, :, two, :])
            else:
                inv_rms = inv_rms_tiles[rho]
                if job is not None:
                    ready = small.tile([P, 1], F32)
                    nc.vector.tensor_scalar(
                        out=ready[:],
                        in0=inv_rms[:, 0:1],
                        scalar1=0.0,
                        scalar2=1.0,
                        op0=ALU.mult,
                        op1=ALU.add,
                    )
                    regroup_rest(job, GPSIMD_SHARE, ready)
                for m, (i, h) in enumerate(pieces):
                    nc.vector.scalar_tensor_tensor(
                        out=stage[:, h, i, :],
                        in0=acc_tiles[(rho, i)][:, h * HEAD : (h + 1) * HEAD],
                        scalar=inv_rms[:, m : m + 1],
                        in1=head_gain,
                        op0=ALU.mult,
                        op1=ALU.mult,
                    )
                nc.sync.dma_start(out=heads, in_=stage[:])

        x_rows = x[0].rearrange("(p i) k -> p i k", i=TOKEN_TILES)
        x_tiles = {}

        def load_x(pair):
            tile = xpool.tile([P, 2, D_MODEL], BF16, tag=f"x{pair}")
            nc.sync.dma_start(out=tile[:], in_=x_rows[:, 2 * pair : 2 * pair + 2, :])
            x_tiles[pair] = tile

        load(0)
        load(1)
        load(2)
        load(3)
        load_x(0)
        scale_rows = const.tile([P, 2 * HEAD], BF16)
        nc.vector.memset(scale_rows[:], 0.0)
        nc.sync.dma_start(out=scale_rows[0:1, 0:HEAD], in_=q_scale.unsqueeze(0))
        nc.sync.dma_start(out=scale_rows[0:1, HEAD:], in_=k_scale.unsqueeze(0))
        load(4)
        load_x(1)
        for s in range(5, RAW_BUFS):
            load(s)

        ident = const.tile([P, P], F32)
        make_identity(nc, ident[:])
        eps = const.tile([P, 1], F32)
        nc.vector.memset(eps[:], EPS)
        first_sqrt = const.tile([P, 1], F32)
        nc.scalar.activation(out=first_sqrt[:], in_=eps[:], func=ACT.Abs_reciprocal_sqrt)
        ones = const.tile([P, P], BF16)
        nc.vector.memset(ones[:], 1.0)

        x_codes = xpool.tile([P, PASSES, TOKENS], U32, align_bytes=64)
        x_scales = xpool.tile([P, PASSES, TOKENS], U8, align_bytes=64)

        def prepare_x(pair):
            for g in range(PASSES):
                xt = psum.tile([P, 2, 2 * P], F32, tag="bank")
                for u in range(2):
                    for half in range(2):
                        words = x_tiles[pair][:, half, g * K_PASS : (g + 1) * K_PASS].bitcast(F32)
                        nc.tensor.transpose(
                            xt[:, u, half * P : (half + 1) * P],
                            words.rearrange("p (q u) -> p q u", u=2)[:, :, u],
                            ident[:],
                        )
                x_grouped = xg_pool.tile([P, 2 * P * PACK], BF16, align_bytes=64)
                nc.scalar.copy(
                    out=x_grouped[:].bitcast(F32).rearrange("p (r u) -> p r u", u=2),
                    in_=xt[:].rearrange("p u r -> p r u"),
                )
                tokens = slice(pair * 2 * P, (pair + 1) * 2 * P)
                nc.vector.quantize_mx(
                    out=x_codes[:, g, tokens].bitcast(FP8X4),
                    scales=x_scales[:, g, tokens],
                    in_=x_grouped[:],
                )

        def spread_gains():
            spread = psum.tile([P, BANK], F32, tag="bank")
            nc.tensor.matmul(out=spread[:], lhsT=ones[:], rhs=scale_rows[:], start=True, stop=True)
            nc.vector.tensor_scalar_add(out=gain[:], in0=spread[:], scalar1=1.0)

        order = []
        for c in range(PAIRED_GROUPS):
            for g in range(PASSES + TRAIL):
                order.extend([(2 * c, g)] if g < PASSES else [])
                order.extend([(2 * c + 1, g - TRAIL)] if g >= TRAIL else [])
        order.extend((rho, g) for rho in range(2 * PAIRED_GROUPS, len(rounds)) for g in range(PASSES))
        done = 0
        later = {}
        with tc.manual_schedule(
            engines={
                mybir.EngineType.PE,
                mybir.EngineType.Activation,
                mybir.EngineType.DVE,
            }
        ):
            for m in range(-REGROUP_AHEAD, len(jobs) + 8):
                if m in (3, 4):
                    prepare_x(m - 3)
                if m == 4:
                    spread_gains()
                job = m + REGROUP_AHEAD
                norms = [rho for step, rho in later.get(m, ()) if step is empty and rho in inv_rms_tiles]
                if job < len(jobs):
                    regroup(job, GPSIMD_SHARE if norms else 0)
                for step, rho in later.get(m, ()):
                    if rho in norms and step is empty:
                        step(rho, job)
                    else:
                        step(rho)
                if job < len(jobs):
                    s, first, width = jobs[job]
                    if first + width == SLAB and s + RAW_BUFS < slabs:
                        load(s + RAW_BUFS)
                if 0 <= m + QUANTISE_AHEAD < len(jobs):
                    quantise(m + QUANTISE_AHEAD)
                while m >= 4 and done < len(order):
                    rho, g = order[done]
                    c, first, width = rounds[rho]
                    if (c * PASSES + g, first) not in code_tiles:
                        break
                    multiply(rho, g)
                    done += 1
                    if g == PASSES - 1:
                        if groups[c][2] is None:
                            later.setdefault(m + 5, []).append((empty, rho))
                        else:
                            n = m + 1 + 3 * (rho % 2) + (1 if c == 0 else 0)
                            later.setdefault(n, []).append((root_mean_squares, rho))
                            later.setdefault(n + 2, []).append((empty, rho))
